import numpy as np
import ml_dtypes


def mxq(x, axis, fmt="e4m3"):
    dtype, down = {"e4m3": (ml_dtypes.float8_e4m3fn, 7), "e5m2": (ml_dtypes.float8_e5m2, 14)}[fmt]
    v = np.moveaxis(np.asarray(x, np.float32).astype(ml_dtypes.bfloat16).astype(np.float64), axis, -1)
    blocks = v.reshape(v.shape[:-1] + (-1, 32))
    amax = np.abs(blocks).max(-1, keepdims=True)
    byte = np.maximum(np.where(amax > 0, np.frexp(amax)[1] - 1 + 127, 0) - down, 1)
    scale = np.exp2(byte - 127.0)
    codes = (blocks / scale).astype(np.float32).astype(dtype).astype(np.float64)
    return np.moveaxis((codes * scale).reshape(v.shape), -1, axis)


WIDE = False


def mx_kscale(k):
    if not WIDE:
        return np.ones(k)
    levels = np.array([10, -10, 5, -5, 0])
    a = np.random.permutation(np.resize(levels, k // 512 * 4)).reshape(k // 512, 4)
    idx = np.arange(k)
    return np.exp2(a[idx // 512, idx % 128 // 32])


BF16 = ml_dtypes.bfloat16


def bf(x):
    return np.asarray(x, np.float32).astype(BF16)


def f64(x):
    return np.asarray(x).astype(np.float64)


E2M1 = np.array([0.0, 0.5, 1.0, 1.5, 2.0, 3.0, 4.0, 6.0, -0.0, -0.5, -1.0, -1.5, -2.0, -3.0, -4.0, -6.0])


def pack_weight(w, fmt):
    k, n = w.shape
    w = f64(bf(w)).reshape(k // 32, 32, n)
    amax = np.abs(w).max(1)
    if fmt == "e4m3":
        byte = np.frexp(amax)[1] - 1 + 127 - 7
    else:
        mant, ex = np.frexp(amax / 6.0)
        byte = np.where(mant > 0.5, ex, ex - 1) + 127
    byte = np.clip(np.where(amax > 0, byte, 1), 1, 254)
    scaled = (w * np.exp2(127.0 - byte)[:, None, :]).reshape(k, n).astype(np.float32)
    by_word = np.ascontiguousarray(scaled.reshape(k // 512, 128, 4, n).transpose(0, 1, 3, 2))
    if fmt == "e4m3":
        words = by_word.astype(ml_dtypes.float8_e4m3fn).view(np.uint8)
    else:
        c = by_word.astype(ml_dtypes.float4_e2m1fn).view(np.uint8) & 0xF
        words = c[..., 0::2] | (c[..., 1::2] << 4)
    return np.ascontiguousarray(words), np.ascontiguousarray(byte.astype(np.uint8).reshape(k // 512, 16, n))


def unpack_weight(words, scales, fmt):
    g, p, n, _ = words.shape
    if fmt == "e4m3":
        vals = np.ascontiguousarray(words).view(ml_dtypes.float8_e4m3fn).astype(np.float64)
    else:
        nib = np.empty((g, p, n, 4), np.uint8)
        nib[..., 0::2] = words & 0xF
        nib[..., 1::2] = words >> 4
        vals = E2M1[nib]
    vals = vals * np.repeat(np.exp2(scales.astype(np.float64) - 127.0), 8, axis=1)[..., None]
    return vals.transpose(0, 1, 3, 2).reshape(g * 512, n)

def pack4(w):
    words, scales = pack_weight(w, "e2m1")
    return words.reshape(words.shape[0], 128, -1), scales


def unpack4(words, scales):
    return unpack_weight(words.reshape(words.shape[0], 128, -1, 2), scales, "e2m1")


LQ, LK, D, H, DK, DV = 1024, 1024, 2048, 4, 128, 128
HV = H * DV
LN_EPS = 1e-5


def setup_inputs():
    s = mx_kscale(HV)
    attn_out = bf(np.random.standard_normal((H, LQ, DV)) * 0.7 * s.reshape(H, DV)[:, None, :])
    residual = bf(np.random.standard_normal((LQ, D)))
    words, scales = pack4(np.random.standard_normal((HV, D)) / np.sqrt(HV) / s[:, None])
    proj_b = bf(np.random.standard_normal(D) * 0.3)
    ln_g = bf(1.0 + 0.1 * np.random.standard_normal(D))
    ln_b = bf(0.1 * np.random.standard_normal(D))
    return {"attn_out": attn_out,
            "residual": residual,
            "proj_w_words": words,
            "proj_w_scales": scales,
            "proj_b": proj_b,
            "ln_g": ln_g,
            "ln_b": ln_b}


def reference(attn_out, residual, proj_w_words, proj_w_scales, proj_b, ln_g, ln_b):
    x = f64(attn_out).transpose(1, 0, 2).reshape(LQ, HV)
    y = (mxq(x, 1, "e4m3") @ unpack4(proj_w_words, proj_w_scales)) + f64(proj_b) + f64(residual)
    mu = y.mean(-1, keepdims=True)
    var = ((y - mu) ** 2).mean(-1, keepdims=True)
    return (y - mu) / np.sqrt(var + LN_EPS) * f64(ln_g) + f64(ln_b)

@@ -1,0 +1,211 @@
+from concourse import mybir
+from concourse.masks import make_identity
+
+F32 = mybir.dt.float32
+BF16 = mybir.dt.bfloat16
+I32 = mybir.dt.int32
+U32 = mybir.dt.uint32
+U8 = mybir.dt.uint8
+FP8X4 = mybir.dt.float8_e4m3fn_x4
+FP4X4 = mybir.dt.float4_e2m1fn_x4
+ALU = mybir.AluOpType
+ACT = mybir.ActivationFunctionType
+
+P = 128
+TOKENS = 1024
+HEADS = 4
+K = 512
+D = 2048
+TILES = TOKENS // P
+BANK = 512
+CHUNKS = D // BANK
+HALF = 2 * BANK
+LN_EPS = 1e-5
+
+FLOPS = 2 * TOKENS * K * D
+
+
+def tile_multiheadattention_pb_kernel(
+    tc, attn_out, residual, proj_w_words, proj_w_scales, proj_b, ln_g, ln_b, out
+):
+    nc = tc.nc
+
+    x_dram = attn_out.rearrange("h (p i) j -> i p h j", i=TILES)
+    res_dram = residual.rearrange("(p i) d -> i p d", i=TILES)
+    out_dram = out.rearrange("(p i) d -> i p d", i=TILES)
+
+    with (
+        tc.tile_pool(name="keep", bufs=1) as keep,
+        tc.tile_pool(name="stage", bufs=2) as stage,
+        tc.tile_pool(name="work", bufs=3) as work,
+        tc.tile_pool(name="stats", bufs=4) as stats,
+        tc.psum_pool(name="vectors", bufs=1) as vectors,
+        tc.psum_pool(name="banks", bufs=4) as banks,
+        tc.manual_schedule(),
+    ):
+        ident = keep.tile([P, P], F32)
+        make_identity(nc, ident[:])
+        rows = keep.tile([P, D], BF16)
+        nc.vector.memset(rows[:].bitcast(I32), 0)
+        w_plane = keep.tile([P, D], U8, align_bytes=64)
+        nc.vector.memset(w_plane[:].bitcast(I32), 0)
+        eps = keep.tile([P, 1], F32)
+        nc.vector.memset(eps[:], LN_EPS)
+        ident_bf = keep.tile([P, P], BF16)
+        nc.vector.tensor_copy(out=ident_bf[:], in_=ident[:])
+        nc.scalar.dma_start(out=rows[0:1, :], in_=proj_b.unsqueeze(0))
+        nc.scalar.dma_start(out=rows[1:2, :], in_=ln_g.unsqueeze(0))
+        nc.scalar.dma_start(out=rows[2:3, :], in_=ln_b.unsqueeze(0))
+        warm = keep.tile([P, 1], F32)
+        nc.scalar.activation(out=warm[:], in_=eps[:], func=ACT.Sqrt)
+
+        x_sb = keep.tile([P, TILES, K], BF16)
+        res_sb = keep.tile([P, TILES, D], BF16)
+        w_words = keep.tile([P, 2 * D], U8, align_bytes=64)
+
+        def load_tokens(i):
+            nc.sync.dma_start(
+                out=x_sb[:, i, :].rearrange("p (h j) -> p h j", h=HEADS), in_=x_dram[i]
+            )
+            nc.sync.dma_start(out=res_sb[:, i, :], in_=res_dram[i])
+
+        load_tokens(0)
+        nc.sync.dma_start(out=w_words[:].bitcast(I32), in_=proj_w_words[0].bitcast(I32))
+        for quadrant in range(4):
+            nc.sync.dma_start(
+                out=w_plane[32 * quadrant : 32 * quadrant + 4, :].bitcast(I32),
+                in_=proj_w_scales[0, 4 * quadrant : 4 * quadrant + 4, :].bitcast(I32),
+            )
+        for i in range(1, TILES):
+            load_tokens(i)
+
+        def spread_row(r, half, target):
+            for c in range(2):
+                nc.tensor.matmul(
+                    out=target[:, c * BANK : (c + 1) * BANK],
+                    lhsT=ident_bf[:, r : r + 1].to_broadcast([P, P]),
+                    rhs=rows[:, half * HALF + c * BANK : half * HALF + (c + 1) * BANK],
+                    start=True,
+                    stop=True,
+                )
+
+        bias_all = keep.tile([P, D], BF16)
+        for half in range(2):
+            bias_ps = banks.tile([P, HALF], BF16, tag="bank")
+            spread_row(0, half, bias_ps)
+            nc.scalar.copy(out=bias_all[:, half * HALF : (half + 1) * HALF], in_=bias_ps[:])
+
+        x_codes = keep.tile([P, TILES, P], U32, align_bytes=64)
+        x_plane = keep.tile([P, TILES, P], U8, align_bytes=64)
+
+        def quantise_tokens(i):
+            x_words = x_sb[:, i, :].bitcast(F32)
+            flipped = banks.tile([P, 2, P], F32, tag="bank")
+            for u in range(2):
+                nc.tensor.transpose(flipped[:, u, :], x_words[:, u : K // 2 : 2], ident[:])
+            grouped = stage.tile([P, 4 * P], BF16, align_bytes=64)
+            nc.scalar.copy(
+                out=grouped[:].bitcast(F32).rearrange("p (r u) -> p r u", u=2),
+                in_=flipped[:].rearrange("p u r -> p r u"),
+            )
+            nc.vector.quantize_mx(
+                out=x_codes[:, i, :].bitcast(FP8X4), scales=x_plane[:, i, :], in_=grouped[:]
+            )
+
+        quantise_tokens(0)
+
+        gain_ps = [vectors.tile([P, HALF], BF16, name="gain%d" % half) for half in range(2)]
+        shift_ps = [vectors.tile([P, HALF], BF16, name="shift%d" % half) for half in range(2)]
+
+        y = {}
+        neg_mean = {}
+        std = {}
+        gained = {}
+
+        def project_and_add(i):
+            adder = nc.vector if i == 0 else nc.gpsimd
+            res_bias = work.tile([P, D], F32, name="res_bias")
+            for c in range(CHUNKS):
+                cols = slice(c * BANK, (c + 1) * BANK)
+                adder.tensor_tensor(
+                    out=res_bias[:, cols], in0=res_sb[:, i, cols], in1=bias_all[:, cols], op=ALU.add
+                )
+            y[i] = work.tile([P, D], F32, name="y")
+            sums = stats.tile([P, CHUNKS], F32, name="sums")
+            for c in range(CHUNKS):
+                cols = slice(c * BANK, (c + 1) * BANK)
+                product = banks.tile([P, BANK], F32, tag="bank")
+                nc.tensor.matmul_mx(
+                    out=product[:],
+                    lhsT=x_codes[:, i, :].bitcast(FP8X4),
+                    lhsT_scale=x_plane[:, i, :],
+                    rhs=w_words[:, 2 * c * BANK : 2 * (c + 1) * BANK].bitcast(FP4X4),
+                    rhs_scale=w_plane[:, cols],
+                    start=True,
+                    stop=True,
+                )
+                nc.vector.scalar_tensor_tensor(
+                    out=y[i][:, cols],
+                    in0=product[:],
+                    scalar=0.0,
+                    in1=res_bias[:, cols],
+                    op0=ALU.add,
+                    op1=ALU.add,
+                    accum_out=sums[:, c : c + 1],
+                )
+            scaled_sums = stats.tile([P, CHUNKS], F32, name="scaled_sums")
+            neg_mean[i] = stats.tile([P, 1], F32, name="neg_mean")
+            nc.scalar.activation(
+                out=scaled_sums[:], in_=sums[:], func=ACT.Copy, scale=-1.0 / D, accum_out=neg_mean[i][:]
+            )
+
+        def centre_and_gain(i):
+            gained[i] = work.tile([P, D], F32, name="gained")
+            for half in range(2):
+                cols = slice(half * HALF, (half + 1) * HALF)
+                nc.vector.scalar_tensor_tensor(
+                    out=gained[i][:, cols],
+                    in0=y[i][:, cols],
+                    scalar=neg_mean[i][:],
+                    in1=gain_ps[half][:],
+                    op0=ALU.add,
+                    op1=ALU.mult,
+                )
+            squares = stage.tile([P, D], BF16, name="squares")
+            sum_sq = stats.tile([P, 1], F32, name="sum_sq")
+            nc.scalar.activation(
+                out=squares[:], in_=y[i][:], func=ACT.Square, bias=neg_mean[i][:], scale=1.0,
+                accum_out=sum_sq[:],
+            )
+            std[i] = stats.tile([P, 1], F32, name="std")
+            nc.scalar.activation(out=std[i][:], in_=sum_sq[:], func=ACT.Sqrt, bias=eps[:], scale=1.0 / D)
+
+        def scale_shift_store(i):
+            rstd = stats.tile([P, 1], F32, name="rstd")
+            nc.vector.reciprocal(out=rstd[:], in_=std[i][:])
+            result = work.tile([P, D], F32, name="result")
+            for half in range(2):
+                cols = slice(half * HALF, (half + 1) * HALF)
+                nc.vector.scalar_tensor_tensor(
+                    out=result[:, cols],
+                    in0=gained[i][:, cols],
+                    scalar=rstd[:],
+                    in1=shift_ps[half][:],
+                    op0=ALU.mult,
+                    op1=ALU.add,
+                )
+                nc.sync.dma_start(out=out_dram[i][:, cols], in_=result[:, cols])
+
+        for i in range(TILES + 1):
+            if i + 1 < TILES:
+                quantise_tokens(i + 1)
+            if i < TILES:
+                project_and_add(i)
+            if i == 0:
+                for half in range(2):
+                    spread_row(1, half, gain_ps[half])
+                    spread_row(2, half, shift_ps[half])
+            if i >= 1:
+                scale_shift_store(i - 1)
+            if i < TILES:
+                centre_and_gain(i)

@@ -123,7 +123,7 @@ def tile_multiheadattention_pb_kernel(
         gained = {}
 
         def project_and_add(i):
-            adder = nc.vector if i == 0 else nc.gpsimd
+            adder = nc.vector
             res_bias = work.tile([P, D], F32, name="res_bias")
             for c in range(CHUNKS):
                 cols = slice(c * BANK, (c + 1) * BANK)

@@ -123,7 +123,7 @@ def tile_multiheadattention_pb_kernel(
         gained = {}
 
         def project_and_add(i):
-            adder = nc.vector
+            adder = nc.vector if i == 0 else nc.gpsimd
             res_bias = work.tile([P, D], F32, name="res_bias")
             for c in range(CHUNKS):
                 cols = slice(c * BANK, (c + 1) * BANK)
@@ -146,9 +146,9 @@ def tile_multiheadattention_pb_kernel(
                 )
                 nc.vector.scalar_tensor_tensor(
                     out=y[i][:, cols],
-                    in0=product[:],
+                    in0=res_bias[:, cols],
                     scalar=0.0,
-                    in1=res_bias[:, cols],
+                    in1=product[:],
                     op0=ALU.add,
                     op1=ALU.add,
                     accum_out=sums[:, c : c + 1],

@@ -19,7 +19,12 @@ D = 2048
 TILES = TOKENS // P
 BANK = 512
 CHUNKS = D // BANK
-HALF = 2 * BANK
+BLOCKS = BANK // P
+GROUP_TILES = 2
+GROUP = GROUP_TILES * P
+UNITS = (TOKENS // GROUP) * CHUNKS
+ROUNDS_A_TILE = UNITS // TILES
+HALF = D // 2
 LN_EPS = 1e-5
 
 FLOPS = 2 * TOKENS * K * D
@@ -38,69 +43,66 @@ def tile_multiheadattention_pb_kernel(
         tc.tile_pool(name="keep", bufs=1) as keep,
         tc.tile_pool(name="stage", bufs=2) as stage,
         tc.tile_pool(name="work", bufs=3) as work,
-        tc.tile_pool(name="stats", bufs=4) as stats,
-        tc.psum_pool(name="vectors", bufs=1) as vectors,
-        tc.psum_pool(name="banks", bufs=4) as banks,
+        tc.tile_pool(name="stats", bufs=TILES) as stats,
+        tc.psum_pool(name="by_feature", bufs=4) as by_feature,
+        tc.psum_pool(name="by_token", bufs=4) as by_token,
         tc.manual_schedule(),
     ):
         ident = keep.tile([P, P], F32)
         make_identity(nc, ident[:])
-        rows = keep.tile([P, D], BF16)
-        nc.vector.memset(rows[:].bitcast(I32), 0)
+        bias_rows = keep.tile([P, P], BF16)
+        nc.vector.memset(bias_rows[:].bitcast(I32), 0)
         w_plane = keep.tile([P, D], U8, align_bytes=64)
         nc.vector.memset(w_plane[:].bitcast(I32), 0)
         eps = keep.tile([P, 1], F32)
         nc.vector.memset(eps[:], LN_EPS)
         ident_bf = keep.tile([P, P], BF16)
         nc.vector.tensor_copy(out=ident_bf[:], in_=ident[:])
-        nc.scalar.dma_start(out=rows[0:1, :], in_=proj_b.unsqueeze(0))
-        nc.scalar.dma_start(out=rows[1:2, :], in_=ln_g.unsqueeze(0))
-        nc.scalar.dma_start(out=rows[2:3, :], in_=ln_b.unsqueeze(0))
+
+        nc.scalar.dma_start(out=bias_rows[0 : D // P, :], in_=proj_b.rearrange("(j p) -> j p", p=P))
         warm = keep.tile([P, 1], F32)
         nc.scalar.activation(out=warm[:], in_=eps[:], func=ACT.Sqrt)
 
         x_sb = keep.tile([P, TILES, K], BF16)
         res_sb = keep.tile([P, TILES, D], BF16)
         w_words = keep.tile([P, 2 * D], U8, align_bytes=64)
+        gain_all = keep.tile([P, D], BF16)
+        shift_all = keep.tile([P, D], BF16)
 
-        def load_tokens(i):
+        def load_x(i):
             nc.sync.dma_start(
                 out=x_sb[:, i, :].rearrange("p (h j) -> p h j", h=HEADS), in_=x_dram[i]
             )
-            nc.sync.dma_start(out=res_sb[:, i, :], in_=res_dram[i])
 
-        load_tokens(0)
-        nc.sync.dma_start(out=w_words[:].bitcast(I32), in_=proj_w_words[0].bitcast(I32))
-        for quadrant in range(4):
-            nc.sync.dma_start(
-                out=w_plane[32 * quadrant : 32 * quadrant + 4, :].bitcast(I32),
-                in_=proj_w_scales[0, 4 * quadrant : 4 * quadrant + 4, :].bitcast(I32),
-            )
-        for i in range(1, TILES):
-            load_tokens(i)
+        for group in range(TOKENS // GROUP):
+            tiles = range(group * GROUP_TILES, (group + 1) * GROUP_TILES)
+            for i in tiles:
+                load_x(i)
+            if group == 0:
+                nc.sync.dma_start(out=w_words[:].bitcast(I32), in_=proj_w_words[0].bitcast(I32))
+                for quadrant in range(4):
+                    nc.sync.dma_start(
+                        out=w_plane[32 * quadrant : 32 * quadrant + 4, :].bitcast(I32),
+                        in_=proj_w_scales[0, 4 * quadrant : 4 * quadrant + 4, :].bitcast(I32),
+                    )
+            if group == 1:
+                nc.sync.dma_start(out=gain_all[:], in_=ln_g.partition_broadcast(P))
+            for i in tiles:
+                nc.sync.dma_start(out=res_sb[:, i, :], in_=res_dram[i])
+            if group == 1:
+                nc.sync.dma_start(out=shift_all[:], in_=ln_b.partition_broadcast(P))
 
-        def spread_row(r, half, target):
-            for c in range(2):
-                nc.tensor.matmul(
-                    out=target[:, c * BANK : (c + 1) * BANK],
-                    lhsT=ident_bf[:, r : r + 1].to_broadcast([P, P]),
-                    rhs=rows[:, half * HALF + c * BANK : half * HALF + (c + 1) * BANK],
-                    start=True,
-                    stop=True,
-                )
+        bias_ps = by_feature.tile([P, P], BF16, tag="bank")
+        nc.tensor.transpose(bias_ps[:], bias_rows[:], ident_bf[:])
+        bias_cols = keep.tile([P, D // P], F32)
+        nc.scalar.copy(out=bias_cols[:], in_=bias_ps[:, 0 : D // P])
 
-        bias_all = keep.tile([P, D], BF16)
-        for half in range(2):
-            bias_ps = banks.tile([P, HALF], BF16, tag="bank")
-            spread_row(0, half, bias_ps)
-            nc.scalar.copy(out=bias_all[:, half * HALF : (half + 1) * HALF], in_=bias_ps[:])
-
-        x_codes = keep.tile([P, TILES, P], U32, align_bytes=64)
-        x_plane = keep.tile([P, TILES, P], U8, align_bytes=64)
+        x_codes = keep.tile([P, TILES * P], U32, align_bytes=64)
+        x_plane = keep.tile([P, TILES * P], U8, align_bytes=64)
 
         def quantise_tokens(i):
             x_words = x_sb[:, i, :].bitcast(F32)
-            flipped = banks.tile([P, 2, P], F32, tag="bank")
+            flipped = by_feature.tile([P, 2, P], F32, tag="bank")
             for u in range(2):
                 nc.tensor.transpose(flipped[:, u, :], x_words[:, u : K // 2 : 2], ident[:])
             grouped = stage.tile([P, 4 * P], BF16, align_bytes=64)
@@ -109,68 +111,75 @@ def tile_multiheadattention_pb_kernel(
                 in_=flipped[:].rearrange("p u r -> p r u"),
             )
             nc.vector.quantize_mx(
-                out=x_codes[:, i, :].bitcast(FP8X4), scales=x_plane[:, i, :], in_=grouped[:]
+                out=x_codes[:, i * P : (i + 1) * P].bitcast(FP8X4),
+                scales=x_plane[:, i * P : (i + 1) * P],
+                in_=grouped[:],
             )
 
-        quantise_tokens(0)
-
-        gain_ps = [vectors.tile([P, HALF], BF16, name="gain%d" % half) for half in range(2)]
-        shift_ps = [vectors.tile([P, HALF], BF16, name="shift%d" % half) for half in range(2)]
-
+        biased = {}
         y = {}
+        sums = {}
         neg_mean = {}
         std = {}
         gained = {}
 
-        def project_and_add(i):
-            adder = nc.vector if i == 0 else nc.gpsimd
-            res_bias = work.tile([P, D], F32, name="res_bias")
-            for c in range(CHUNKS):
-                cols = slice(c * BANK, (c + 1) * BANK)
-                adder.tensor_tensor(
-                    out=res_bias[:, cols], in0=res_sb[:, i, cols], in1=bias_all[:, cols], op=ALU.add
-                )
-            y[i] = work.tile([P, D], F32, name="y")
-            sums = stats.tile([P, CHUNKS], F32, name="sums")
-            for c in range(CHUNKS):
-                cols = slice(c * BANK, (c + 1) * BANK)
-                product = banks.tile([P, BANK], F32, tag="bank")
+        def project(unit):
+            group, chunk = divmod(unit, CHUNKS)
+            tokens = slice(group * GROUP, (group + 1) * GROUP)
+            biased[unit] = work.tile([P, BLOCKS, GROUP], F32, name="biased")
+            for b in range(BLOCKS):
+                j = chunk * BLOCKS + b
+                product = by_feature.tile([P, GROUP], F32, tag="bank")
                 nc.tensor.matmul_mx(
                     out=product[:],
-                    lhsT=x_codes[:, i, :].bitcast(FP8X4),
-                    lhsT_scale=x_plane[:, i, :],
-                    rhs=w_words[:, 2 * c * BANK : 2 * (c + 1) * BANK].bitcast(FP4X4),
-                    rhs_scale=w_plane[:, cols],
+                    lhsT=w_words[:, 2 * j * P : 2 * (j + 1) * P].bitcast(FP4X4),
+                    lhsT_scale=w_plane[:, j * P : (j + 1) * P],
+                    rhs=x_codes[:, tokens].bitcast(FP8X4),
+                    rhs_scale=x_plane[:, tokens],
                     start=True,
                     stop=True,
                 )
+                nc.scalar.activation(
+                    out=biased[unit][:, b, :], in_=product[:], func=ACT.Identity,
+                    bias=bias_cols[:, j : j + 1], scale=1.0,
+                )
+
+        def add_residual(unit):
+            group, chunk = divmod(unit, CHUNKS)
+            cols = slice(chunk * BANK, (chunk + 1) * BANK)
+            for a in range(GROUP_TILES):
+                i = group * GROUP_TILES + a
+                if chunk == 0:
+                    y[i] = work.tile([P, D], F32, name="y", bufs=TILES)
+                    sums[i] = stats.tile([P, CHUNKS], F32, name="sums")
+                turned = by_token.tile([P, BANK], F32)
+                for b in range(BLOCKS):
+                    nc.tensor.transpose(
+                        turned[:, b * P : (b + 1) * P], biased[unit][:, b, a * P : (a + 1) * P], ident[:]
+                    )
                 nc.vector.scalar_tensor_tensor(
                     out=y[i][:, cols],
-                    in0=res_bias[:, cols],
+                    in0=turned[:],
                     scalar=0.0,
-                    in1=product[:],
+                    in1=res_sb[:, i, cols],
                     op0=ALU.add,
                     op1=ALU.add,
-                    accum_out=sums[:, c : c + 1],
+                    accum_out=sums[i][:, chunk : chunk + 1],
                 )
-            scaled_sums = stats.tile([P, CHUNKS], F32, name="scaled_sums")
-            neg_mean[i] = stats.tile([P, 1], F32, name="neg_mean")
-            nc.scalar.activation(
-                out=scaled_sums[:], in_=sums[:], func=ACT.Copy, scale=-1.0 / D, accum_out=neg_mean[i][:]
-            )
+                if chunk == CHUNKS - 1:
+                    scaled_sums = stats.tile([P, CHUNKS], F32, name="scaled_sums")
+                    neg_mean[i] = stats.tile([P, 1], F32, name="neg_mean")
+                    nc.scalar.activation(
+                        out=scaled_sums[:], in_=sums[i][:], func=ACT.Copy, scale=-1.0 / D,
+                        accum_out=neg_mean[i][:],
+                    )
 
         def centre_and_gain(i):
             gained[i] = work.tile([P, D], F32, name="gained")
-            for half in range(2):
-                cols = slice(half * HALF, (half + 1) * HALF)
-                nc.vector.scalar_tensor_tensor(
-                    out=gained[i][:, cols],
-                    in0=y[i][:, cols],
-                    scalar=neg_mean[i][:],
-                    in1=gain_ps[half][:],
-                    op0=ALU.add,
-                    op1=ALU.mult,
-                )
+            nc.vector.scalar_tensor_tensor(
+                out=gained[i][:], in0=y[i][:], scalar=neg_mean[i][:], in1=gain_all[:],
+                op0=ALU.add, op1=ALU.mult,
+            )
             squares = stage.tile([P, D], BF16, name="squares")
             sum_sq = stats.tile([P, 1], F32, name="sum_sq")
             nc.scalar.activation(
@@ -187,25 +196,26 @@ def tile_multiheadattention_pb_kernel(
             for half in range(2):
                 cols = slice(half * HALF, (half + 1) * HALF)
                 nc.vector.scalar_tensor_tensor(
-                    out=result[:, cols],
-                    in0=gained[i][:, cols],
-                    scalar=rstd[:],
-                    in1=shift_ps[half][:],
-                    op0=ALU.mult,
-                    op1=ALU.add,
+                    out=result[:, cols], in0=gained[i][:, cols], scalar=rstd[:], in1=shift_all[:, cols],
+                    op0=ALU.mult, op1=ALU.add,
                 )
                 nc.sync.dma_start(out=out_dram[i][:, cols], in_=result[:, cols])
 
-        for i in range(TILES + 1):
-            if i + 1 < TILES:
-                quantise_tokens(i + 1)
-            if i < TILES:
-                project_and_add(i)
-            if i == 0:
-                for half in range(2):
-                    spread_row(1, half, gain_ps[half])
-                    spread_row(2, half, shift_ps[half])
-            if i >= 1:
-                scale_shift_store(i - 1)
-            if i < TILES:
+        first_centre = CHUNKS
+        first_finish = CHUNKS + ROUNDS_A_TILE + 1
+        for i in range(GROUP_TILES):
+            quantise_tokens(i)
+        project(0)
+        for r in range(first_finish + ROUNDS_A_TILE * (TILES - 1) + 1):
+            if r + GROUP_TILES < TILES:
+                quantise_tokens(r + GROUP_TILES)
+            if r + 1 < UNITS:
+                project(r + 1)
+            if r < UNITS:
+                add_residual(r)
+            i, odd = divmod(r - first_centre, ROUNDS_A_TILE)
+            if odd == 0 and 0 <= i < TILES:
                 centre_and_gain(i)
+            i, odd = divmod(r - first_finish, ROUNDS_A_TILE)
+            if odd == 0 and 0 <= i < TILES:
+                scale_shift_store(i)

@@ -18,14 +18,17 @@ K = 512
 D = 2048
 TILES = TOKENS // P
 BANK = 512
+BANK_BF = 2 * BANK
 CHUNKS = D // BANK
 BLOCKS = BANK // P
 GROUP_TILES = 2
 GROUP = GROUP_TILES * P
-UNITS = (TOKENS // GROUP) * CHUNKS
-ROUNDS_A_TILE = UNITS // TILES
-HALF = D // 2
+GROUPS = TOKENS // GROUP
+UNITS = GROUPS * CHUNKS
 LN_EPS = 1e-5
+POOL_COLS = 768
+POOL_COLS_LAST = 384
+POOL_FROM = D - POOL_COLS
 
 FLOPS = 2 * TOKENS * K * D
 
@@ -44,14 +47,17 @@ def tile_multiheadattention_pb_kernel(
         tc.tile_pool(name="stage", bufs=2) as stage,
         tc.tile_pool(name="work", bufs=3) as work,
         tc.tile_pool(name="stats", bufs=TILES) as stats,
-        tc.psum_pool(name="by_feature", bufs=4) as by_feature,
-        tc.psum_pool(name="by_token", bufs=4) as by_token,
+        tc.psum_pool(name="spread", bufs=1) as spread,
+        tc.psum_pool(name="by_feature", bufs=2) as by_feature,
+        tc.psum_pool(name="by_token", bufs=2) as by_token,
         tc.manual_schedule(),
     ):
         ident = keep.tile([P, P], F32)
         make_identity(nc, ident[:])
         bias_rows = keep.tile([P, P], BF16)
         nc.vector.memset(bias_rows[:].bitcast(I32), 0)
+        norm_rows = keep.tile([P, BANK], BF16)
+        nc.vector.memset(norm_rows[:].bitcast(I32), 0)
         w_plane = keep.tile([P, D], U8, align_bytes=64)
         nc.vector.memset(w_plane[:].bitcast(I32), 0)
         eps = keep.tile([P, 1], F32)
@@ -60,89 +66,115 @@ def tile_multiheadattention_pb_kernel(
         nc.vector.tensor_copy(out=ident_bf[:], in_=ident[:])
 
         nc.scalar.dma_start(out=bias_rows[0 : D // P, :], in_=proj_b.rearrange("(j p) -> j p", p=P))
+        nc.scalar.dma_start(out=norm_rows[0:CHUNKS, :], in_=ln_g.rearrange("(c n) -> c n", n=BANK))
+        nc.scalar.dma_start(
+            out=norm_rows[CHUNKS : 2 * CHUNKS, :], in_=ln_b.rearrange("(c n) -> c n", n=BANK)
+        )
         warm = keep.tile([P, 1], F32)
-        nc.scalar.activation(out=warm[:], in_=eps[:], func=ACT.Sqrt)
+        nc.scalar.activation(out=warm[:], in_=eps[:], func=ACT.Abs_reciprocal_sqrt)
 
         x_sb = keep.tile([P, TILES, K], BF16)
         res_sb = keep.tile([P, TILES, D], BF16)
         w_words = keep.tile([P, 2 * D], U8, align_bytes=64)
-        gain_all = keep.tile([P, D], BF16)
-        shift_all = keep.tile([P, D], BF16)
 
         def load_x(i):
             nc.sync.dma_start(
                 out=x_sb[:, i, :].rearrange("p (h j) -> p h j", h=HEADS), in_=x_dram[i]
             )
 
-        for group in range(TOKENS // GROUP):
+        def load_words(chunk):
+            cols = slice(chunk * 2 * BANK, (chunk + 1) * 2 * BANK)
+            nc.sync.dma_start(out=w_words[:, cols].bitcast(I32), in_=proj_w_words[0][:, cols].bitcast(I32))
+
+        for group in range(GROUPS):
             tiles = range(group * GROUP_TILES, (group + 1) * GROUP_TILES)
             for i in tiles:
                 load_x(i)
             if group == 0:
-                nc.sync.dma_start(out=w_words[:].bitcast(I32), in_=proj_w_words[0].bitcast(I32))
+                load_words(0)
                 for quadrant in range(4):
                     nc.sync.dma_start(
                         out=w_plane[32 * quadrant : 32 * quadrant + 4, :].bitcast(I32),
                         in_=proj_w_scales[0, 4 * quadrant : 4 * quadrant + 4, :].bitcast(I32),
                     )
-            if group == 1:
-                nc.sync.dma_start(out=gain_all[:], in_=ln_g.partition_broadcast(P))
+                for chunk in range(1, CHUNKS):
+                    load_words(chunk)
             for i in tiles:
                 nc.sync.dma_start(out=res_sb[:, i, :], in_=res_dram[i])
-            if group == 1:
-                nc.sync.dma_start(out=shift_all[:], in_=ln_b.partition_broadcast(P))
 
-        bias_ps = by_feature.tile([P, P], BF16, tag="bank")
+        bias_ps = by_feature.tile([P, P], BF16, tag="product")
         nc.tensor.transpose(bias_ps[:], bias_rows[:], ident_bf[:])
         bias_cols = keep.tile([P, D // P], F32)
         nc.scalar.copy(out=bias_cols[:], in_=bias_ps[:, 0 : D // P])
 
+        gain_ps = [spread.tile([P, BANK_BF], BF16, name="gain_ps%d" % h) for h in range(2)]
+        shift_ps = [spread.tile([P, BANK_BF], BF16, name="shift_ps%d" % h) for h in range(2)]
+
+        def spread_rows(banks, first_row):
+            for chunk in range(CHUNKS):
+                row = first_row + chunk
+                half, part = divmod(chunk, 2)
+                nc.tensor.matmul(
+                    out=banks[half][:, part * BANK : (part + 1) * BANK],
+                    lhsT=ident_bf[:, row : row + 1].to_broadcast([P, P]),
+                    rhs=norm_rows[:],
+                    start=True,
+                    stop=True,
+                )
+
         x_codes = keep.tile([P, TILES * P], U32, align_bytes=64)
         x_plane = keep.tile([P, TILES * P], U8, align_bytes=64)
+        grouped = {}
 
-        def quantise_tokens(i):
-            x_words = x_sb[:, i, :].bitcast(F32)
-            flipped = by_feature.tile([P, 2, P], F32, tag="bank")
-            for u in range(2):
-                nc.tensor.transpose(flipped[:, u, :], x_words[:, u : K // 2 : 2], ident[:])
-            grouped = stage.tile([P, 4 * P], BF16, align_bytes=64)
+        def turn_tokens(group):
+            flipped = by_token.tile([P, GROUP_TILES, 2, P], F32, tag="turned")
+            for a in range(GROUP_TILES):
+                x_words = x_sb[:, group * GROUP_TILES + a, :].bitcast(F32)
+                for u in range(2):
+                    nc.tensor.transpose(flipped[:, a, u, :], x_words[:, u : K // 2 : 2], ident[:])
+            grouped[group] = stage.tile([P, GROUP * 4], BF16, align_bytes=64, name="grouped")
             nc.scalar.copy(
-                out=grouped[:].bitcast(F32).rearrange("p (r u) -> p r u", u=2),
-                in_=flipped[:].rearrange("p u r -> p r u"),
+                out=grouped[group][:].bitcast(F32).rearrange("p (a r u) -> p a r u", a=GROUP_TILES, u=2),
+                in_=flipped[:].rearrange("p a u r -> p a r u"),
             )
+
+        def quantise_tokens(group):
+            tokens = slice(group * GROUP, (group + 1) * GROUP)
             nc.vector.quantize_mx(
-                out=x_codes[:, i * P : (i + 1) * P].bitcast(FP8X4),
-                scales=x_plane[:, i * P : (i + 1) * P],
-                in_=grouped[:],
+                out=x_codes[:, tokens].bitcast(FP8X4), scales=x_plane[:, tokens], in_=grouped[group][:]
             )
 
         biased = {}
         y = {}
         sums = {}
         neg_mean = {}
-        std = {}
+        rstd = {}
         gained = {}
+        result = {}
 
         def project(unit):
             group, chunk = divmod(unit, CHUNKS)
             tokens = slice(group * GROUP, (group + 1) * GROUP)
             biased[unit] = work.tile([P, BLOCKS, GROUP], F32, name="biased")
-            for b in range(BLOCKS):
-                j = chunk * BLOCKS + b
-                product = by_feature.tile([P, GROUP], F32, tag="bank")
-                nc.tensor.matmul_mx(
-                    out=product[:],
-                    lhsT=w_words[:, 2 * j * P : 2 * (j + 1) * P].bitcast(FP4X4),
-                    lhsT_scale=w_plane[:, j * P : (j + 1) * P],
-                    rhs=x_codes[:, tokens].bitcast(FP8X4),
-                    rhs_scale=x_plane[:, tokens],
-                    start=True,
-                    stop=True,
-                )
-                nc.scalar.activation(
-                    out=biased[unit][:, b, :], in_=product[:], func=ACT.Identity,
-                    bias=bias_cols[:, j : j + 1], scale=1.0,
-                )
+            for pair in range(BLOCKS // 2):
+                product = by_feature.tile([P, 2, GROUP], F32, tag="product")
+                for e in range(2):
+                    j = chunk * BLOCKS + 2 * pair + e
+                    nc.tensor.matmul_mx(
+                        out=product[:, e, :],
+                        lhsT=w_words[:, 2 * j * P : 2 * (j + 1) * P].bitcast(FP4X4),
+                        lhsT_scale=w_plane[:, j * P : (j + 1) * P],
+                        rhs=x_codes[:, tokens].bitcast(FP8X4),
+                        rhs_scale=x_plane[:, tokens],
+                        start=True,
+                        stop=True,
+                    )
+                for e in range(2):
+                    j = chunk * BLOCKS + 2 * pair + e
+                    nc.scalar.activation(
+                        out=biased[unit][:, 2 * pair + e, :], in_=product[:, e, :], func=ACT.Identity,
+                        bias=bias_cols[:, j : j + 1], scale=1.0,
+                    )
 
         def add_residual(unit):
             group, chunk = divmod(unit, CHUNKS)
@@ -152,7 +184,7 @@ def tile_multiheadattention_pb_kernel(
                 if chunk == 0:
                     y[i] = work.tile([P, D], F32, name="y", bufs=TILES)
                     sums[i] = stats.tile([P, CHUNKS], F32, name="sums")
-                turned = by_token.tile([P, BANK], F32)
+                turned = by_token.tile([P, BANK], F32, tag="turned")
                 for b in range(BLOCKS):
                     nc.tensor.transpose(
                         turned[:, b * P : (b + 1) * P], biased[unit][:, b, a * P : (a + 1) * P], ident[:]
@@ -174,48 +206,89 @@ def tile_multiheadattention_pb_kernel(
                         accum_out=neg_mean[i][:],
                     )
 
+        def pool_from(i):
+            return D - (POOL_COLS_LAST if i // GROUP_TILES == GROUPS - 1 else POOL_COLS)
+
+        def vector_parts(i):
+            end = pool_from(i)
+            return [(lo, min(lo + BANK_BF, end)) for lo in range(0, end, BANK_BF)]
+
         def centre_and_gain(i):
             gained[i] = work.tile([P, D], F32, name="gained")
-            nc.vector.scalar_tensor_tensor(
-                out=gained[i][:], in0=y[i][:], scalar=neg_mean[i][:], in1=gain_all[:],
-                op0=ALU.add, op1=ALU.mult,
-            )
+            for lo, hi in vector_parts(i):
+                nc.vector.scalar_tensor_tensor(
+                    out=gained[i][:, lo:hi], in0=y[i][:, lo:hi], scalar=neg_mean[i][:],
+                    in1=gain_ps[lo // BANK_BF][:, 0 : hi - lo],
+                    op0=ALU.add, op1=ALU.mult,
+                )
+
+        def deviation(i):
             squares = stage.tile([P, D], BF16, name="squares")
             sum_sq = stats.tile([P, 1], F32, name="sum_sq")
             nc.scalar.activation(
                 out=squares[:], in_=y[i][:], func=ACT.Square, bias=neg_mean[i][:], scale=1.0,
                 accum_out=sum_sq[:],
             )
-            std[i] = stats.tile([P, 1], F32, name="std")
-            nc.scalar.activation(out=std[i][:], in_=sum_sq[:], func=ACT.Sqrt, bias=eps[:], scale=1.0 / D)
+            rstd[i] = stats.tile([P, 1], F32, name="rstd")
+            nc.scalar.activation(
+                out=rstd[i][:], in_=sum_sq[:], func=ACT.Abs_reciprocal_sqrt, bias=eps[:], scale=1.0 / D
+            )
+
+        def pool_columns(i):
+            result[i] = work.tile([P, D], F32, name="result", bufs=4)
+            first = pool_from(i)
+            mine = result[i][:, first:D]
+            nc.gpsimd.tensor_scalar(
+                out=mine, in0=y[i][:, first:D], scalar1=neg_mean[i][:], scalar2=rstd[i][:],
+                op0=ALU.add, op1=ALU.mult,
+            )
+            nc.gpsimd.tensor_tensor(out=mine, in0=mine, in1=gain_sb[:, first - POOL_FROM :], op=ALU.mult)
+            nc.gpsimd.tensor_tensor(out=mine, in0=mine, in1=shift_sb[:, first - POOL_FROM :], op=ALU.add)
 
         def scale_shift_store(i):
-            rstd = stats.tile([P, 1], F32, name="rstd")
-            nc.vector.reciprocal(out=rstd[:], in_=std[i][:])
-            result = work.tile([P, D], F32, name="result")
-            for half in range(2):
-                cols = slice(half * HALF, (half + 1) * HALF)
+            for lo, hi in vector_parts(i):
                 nc.vector.scalar_tensor_tensor(
-                    out=result[:, cols], in0=gained[i][:, cols], scalar=rstd[:], in1=shift_all[:, cols],
+                    out=result[i][:, lo:hi], in0=gained[i][:, lo:hi], scalar=rstd[i][:],
+                    in1=shift_ps[lo // BANK_BF][:, 0 : hi - lo],
                     op0=ALU.mult, op1=ALU.add,
                 )
-                nc.sync.dma_start(out=out_dram[i][:, cols], in_=result[:, cols])
+                nc.sync.dma_start(out=out_dram[i][:, lo:hi], in_=result[i][:, lo:hi])
+            first = pool_from(i)
+            nc.sync.dma_start(out=out_dram[i][:, first:D], in_=result[i][:, first:D])
 
-        first_centre = CHUNKS
-        first_finish = CHUNKS + ROUNDS_A_TILE + 1
-        for i in range(GROUP_TILES):
-            quantise_tokens(i)
+        turn_tokens(0)
+        spread_rows(gain_ps, 0)
+        quantise_tokens(0)
         project(0)
-        for r in range(first_finish + ROUNDS_A_TILE * (TILES - 1) + 1):
-            if r + GROUP_TILES < TILES:
-                quantise_tokens(r + GROUP_TILES)
+        spread_rows(shift_ps, CHUNKS)
+        gain_sb = keep.tile([P, POOL_COLS], BF16)
+        shift_sb = keep.tile([P, POOL_COLS], BF16)
+
+        for r in range(UNITS + CHUNKS):
+            ahead = r // CHUNKS + 1
+            if r % CHUNKS == 1 and ahead < GROUPS:
+                turn_tokens(ahead)
             if r + 1 < UNITS:
                 project(r + 1)
+            if r == 1:
+                nc.scalar.copy(out=gain_sb[:], in_=gain_ps[1][:, POOL_FROM - BANK_BF :])
+                nc.scalar.copy(out=shift_sb[:], in_=shift_ps[1][:, POOL_FROM - BANK_BF :])
+            if r % CHUNKS == 2 and ahead < GROUPS:
+                quantise_tokens(ahead)
             if r < UNITS:
                 add_residual(r)
-            i, odd = divmod(r - first_centre, ROUNDS_A_TILE)
-            if odd == 0 and 0 <= i < TILES:
-                centre_and_gain(i)
-            i, odd = divmod(r - first_finish, ROUNDS_A_TILE)
-            if odd == 0 and 0 <= i < TILES:
-                scale_shift_store(i)
+            group, step = divmod(r - CHUNKS, CHUNKS)
+            if group >= 0:
+                first = group * GROUP_TILES
+                if step == 0:
+                    centre_and_gain(first)
+                    deviation(first)
+                if step == 1:
+                    centre_and_gain(first + 1)
+                    deviation(first + 1)
+                    pool_columns(first)
+                if step == 2:
+                    pool_columns(first + 1)
+                    scale_shift_store(first)
+                if step == 3:
+                    scale_shift_store(first + 1)

@@ -29,6 +29,7 @@ LN_EPS = 1e-5
 POOL_COLS = 768
 POOL_COLS_LAST = 384
 POOL_FROM = D - POOL_COLS
+VECTOR_MOST = D - POOL_COLS_LAST
 
 FLOPS = 2 * TOKENS * K * D
 
@@ -86,21 +87,28 @@ def tile_multiheadattention_pb_kernel(
             cols = slice(chunk * 2 * BANK, (chunk + 1) * 2 * BANK)
             nc.sync.dma_start(out=w_words[:, cols].bitcast(I32), in_=proj_w_words[0][:, cols].bitcast(I32))
 
+        def load_residual(i):
+            nc.sync.dma_start(out=res_sb[:, i, :], in_=res_dram[i])
+
         for group in range(GROUPS):
-            tiles = range(group * GROUP_TILES, (group + 1) * GROUP_TILES)
-            for i in tiles:
+            for i in range(group * GROUP_TILES, (group + 1) * GROUP_TILES):
                 load_x(i)
+            load_words(group)
             if group == 0:
-                load_words(0)
                 for quadrant in range(4):
                     nc.sync.dma_start(
                         out=w_plane[32 * quadrant : 32 * quadrant + 4, :].bitcast(I32),
                         in_=proj_w_scales[0, 4 * quadrant : 4 * quadrant + 4, :].bitcast(I32),
                     )
-                for chunk in range(1, CHUNKS):
-                    load_words(chunk)
-            for i in tiles:
-                nc.sync.dma_start(out=res_sb[:, i, :], in_=res_dram[i])
+            if group == 1:
+                for i in range(GROUP_TILES):
+                    load_residual(i)
+        for i in range(GROUP_TILES, TILES):
+            load_residual(i)
+        gain_sb = keep.tile([P, POOL_COLS], BF16)
+        shift_sb = keep.tile([P, POOL_COLS], BF16)
+        nc.sync.dma_start(out=gain_sb[:], in_=ln_g[POOL_FROM:D].partition_broadcast(P))
+        nc.sync.dma_start(out=shift_sb[:], in_=ln_b[POOL_FROM:D].partition_broadcast(P))
 
         bias_ps = by_feature.tile([P, P], BF16, tag="product")
         nc.tensor.transpose(bias_ps[:], bias_rows[:], ident_bf[:])
@@ -114,10 +122,11 @@ def tile_multiheadattention_pb_kernel(
             for chunk in range(CHUNKS):
                 row = first_row + chunk
                 half, part = divmod(chunk, 2)
+                width = min(BANK, VECTOR_MOST - chunk * BANK)
                 nc.tensor.matmul(
-                    out=banks[half][:, part * BANK : (part + 1) * BANK],
+                    out=banks[half][:, part * BANK : part * BANK + width],
                     lhsT=ident_bf[:, row : row + 1].to_broadcast([P, P]),
-                    rhs=norm_rows[:],
+                    rhs=norm_rows[:, 0:width],
                     start=True,
                     stop=True,
                 )
@@ -126,16 +135,22 @@ def tile_multiheadattention_pb_kernel(
         x_plane = keep.tile([P, TILES * P], U8, align_bytes=64)
         grouped = {}
 
-        def turn_tokens(group):
-            flipped = by_token.tile([P, GROUP_TILES, 2, P], F32, tag="turned")
+        flipped = {}
+
+        def flip_tokens(group):
+            flipped[group] = by_token.tile([P, GROUP_TILES, 2, P], F32, name="flipped", tag="turned")
             for a in range(GROUP_TILES):
                 x_words = x_sb[:, group * GROUP_TILES + a, :].bitcast(F32)
                 for u in range(2):
-                    nc.tensor.transpose(flipped[:, a, u, :], x_words[:, u : K // 2 : 2], ident[:])
+                    nc.tensor.transpose(
+                        flipped[group][:, a, u, :], x_words[:, u : K // 2 : 2], ident[:]
+                    )
+
+        def gather_tokens(group):
             grouped[group] = stage.tile([P, GROUP * 4], BF16, align_bytes=64, name="grouped")
             nc.scalar.copy(
                 out=grouped[group][:].bitcast(F32).rearrange("p (a r u) -> p a r u", a=GROUP_TILES, u=2),
-                in_=flipped[:].rearrange("p a u r -> p a r u"),
+                in_=flipped[group][:].rearrange("p a u r -> p a r u"),
             )
 
         def quantise_tokens(group):
@@ -256,25 +271,26 @@ def tile_multiheadattention_pb_kernel(
             first = pool_from(i)
             nc.sync.dma_start(out=out_dram[i][:, first:D], in_=result[i][:, first:D])
 
-        turn_tokens(0)
-        spread_rows(gain_ps, 0)
+        flip_tokens(0)
+        gather_tokens(0)
+        flip_tokens(1)
         quantise_tokens(0)
         project(0)
-        spread_rows(shift_ps, CHUNKS)
-        gain_sb = keep.tile([P, POOL_COLS], BF16)
-        shift_sb = keep.tile([P, POOL_COLS], BF16)
+        gather_tokens(1)
+        quantise_tokens(1)
 
         for r in range(UNITS + CHUNKS):
-            ahead = r // CHUNKS + 1
-            if r % CHUNKS == 1 and ahead < GROUPS:
-                turn_tokens(ahead)
+            if 2 <= r + 1 < GROUPS:
+                flip_tokens(r + 1)
+                gather_tokens(r + 1)
+            if r == CHUNKS:
+                spread_rows(gain_ps, 0)
+            if r == CHUNKS + 1:
+                spread_rows(shift_ps, CHUNKS)
             if r + 1 < UNITS:
                 project(r + 1)
-            if r == 1:
-                nc.scalar.copy(out=gain_sb[:], in_=gain_ps[1][:, POOL_FROM - BANK_BF :])
-                nc.scalar.copy(out=shift_sb[:], in_=shift_ps[1][:, POOL_FROM - BANK_BF :])
-            if r % CHUNKS == 2 and ahead < GROUPS:
-                quantise_tokens(ahead)
+            if 2 <= r < GROUPS:
+                quantise_tokens(r)
             if r < UNITS:
                 add_residual(r)
             group, step = divmod(r - CHUNKS, CHUNKS)

@@ -66,9 +66,9 @@ def tile_multiheadattention_pb_kernel(
         ident_bf = keep.tile([P, P], BF16)
         nc.vector.tensor_copy(out=ident_bf[:], in_=ident[:])
 
-        nc.scalar.dma_start(out=bias_rows[0 : D // P, :], in_=proj_b.rearrange("(j p) -> j p", p=P))
-        nc.scalar.dma_start(out=norm_rows[0:CHUNKS, :], in_=ln_g.rearrange("(c n) -> c n", n=BANK))
-        nc.scalar.dma_start(
+        nc.gpsimd.dma_start(out=bias_rows[0 : D // P, :], in_=proj_b.rearrange("(j p) -> j p", p=P))
+        nc.gpsimd.dma_start(out=norm_rows[0:CHUNKS, :], in_=ln_g.rearrange("(c n) -> c n", n=BANK))
+        nc.gpsimd.dma_start(
             out=norm_rows[CHUNKS : 2 * CHUNKS, :], in_=ln_b.rearrange("(c n) -> c n", n=BANK)
         )
         warm = keep.tile([P, 1], F32)
@@ -90,19 +90,22 @@ def tile_multiheadattention_pb_kernel(
         def load_residual(i):
             nc.sync.dma_start(out=res_sb[:, i, :], in_=res_dram[i])
 
-        for group in range(GROUPS):
+        for i in range(GROUP_TILES):
+            load_x(i)
+        load_words(0)
+        for quadrant in range(4):
+            nc.sync.dma_start(
+                out=w_plane[32 * quadrant : 32 * quadrant + 4, :].bitcast(I32),
+                in_=proj_w_scales[0, 4 * quadrant : 4 * quadrant + 4, :].bitcast(I32),
+            )
+        load_residual(0)
+        load_words(1)
+        load_residual(1)
+        for group in range(1, GROUPS):
             for i in range(group * GROUP_TILES, (group + 1) * GROUP_TILES):
                 load_x(i)
-            load_words(group)
-            if group == 0:
-                for quadrant in range(4):
-                    nc.sync.dma_start(
-                        out=w_plane[32 * quadrant : 32 * quadrant + 4, :].bitcast(I32),
-                        in_=proj_w_scales[0, 4 * quadrant : 4 * quadrant + 4, :].bitcast(I32),
-                    )
-            if group == 1:
-                for i in range(GROUP_TILES):
-                    load_residual(i)
+            if group + 1 < CHUNKS:
+                load_words(group + 1)
         for i in range(GROUP_TILES, TILES):
             load_residual(i)
         gain_sb = keep.tile([P, POOL_COLS], BF16)
@@ -110,10 +113,12 @@ def tile_multiheadattention_pb_kernel(
         nc.sync.dma_start(out=gain_sb[:], in_=ln_g[POOL_FROM:D].partition_broadcast(P))
         nc.sync.dma_start(out=shift_sb[:], in_=ln_b[POOL_FROM:D].partition_broadcast(P))
 
-        bias_ps = by_feature.tile([P, P], BF16, tag="product")
-        nc.tensor.transpose(bias_ps[:], bias_rows[:], ident_bf[:])
         bias_cols = keep.tile([P, D // P], F32)
-        nc.scalar.copy(out=bias_cols[:], in_=bias_ps[:, 0 : D // P])
+
+        def turn_bias():
+            bias_ps = by_feature.tile([P, P], BF16, tag="product")
+            nc.tensor.transpose(bias_ps[:], bias_rows[:], ident_bf[:])
+            nc.scalar.copy(out=bias_cols[:], in_=bias_ps[:, 0 : D // P])
 
         gain_ps = [spread.tile([P, BANK_BF], BF16, name="gain_ps%d" % h) for h in range(2)]
         shift_ps = [spread.tile([P, BANK_BF], BF16, name="shift_ps%d" % h) for h in range(2)]
@@ -273,14 +278,12 @@ def tile_multiheadattention_pb_kernel(
 
         flip_tokens(0)
         gather_tokens(0)
-        flip_tokens(1)
+        turn_bias()
         quantise_tokens(0)
         project(0)
-        gather_tokens(1)
-        quantise_tokens(1)
 
         for r in range(UNITS + CHUNKS):
-            if 2 <= r + 1 < GROUPS:
+            if r + 1 < GROUPS:
                 flip_tokens(r + 1)
                 gather_tokens(r + 1)
             if r == CHUNKS:
@@ -289,7 +292,7 @@ def tile_multiheadattention_pb_kernel(
                 spread_rows(shift_ps, CHUNKS)
             if r + 1 < UNITS:
                 project(r + 1)
-            if 2 <= r < GROUPS:
+            if 1 <= r < GROUPS:
                 quantise_tokens(r)
             if r < UNITS:
                 add_residual(r)

@@ -26,10 +26,11 @@ GROUP = GROUP_TILES * P
 GROUPS = TOKENS // GROUP
 UNITS = GROUPS * CHUNKS
 LN_EPS = 1e-5
-POOL_COLS = 768
+POOL_COLS = 640
 POOL_COLS_LAST = 384
 POOL_FROM = D - POOL_COLS
 VECTOR_MOST = D - POOL_COLS_LAST
+AHEAD = 2
 
 FLOPS = 2 * TOKENS * K * D
 
@@ -175,7 +176,7 @@ def tile_multiheadattention_pb_kernel(
         def project(unit):
             group, chunk = divmod(unit, CHUNKS)
             tokens = slice(group * GROUP, (group + 1) * GROUP)
-            biased[unit] = work.tile([P, BLOCKS, GROUP], F32, name="biased")
+            biased[unit] = work.tile([P, BLOCKS, GROUP], F32, name="biased", bufs=AHEAD + 2)
             for pair in range(BLOCKS // 2):
                 product = by_feature.tile([P, 2, GROUP], F32, tag="product")
                 for e in range(2):
@@ -280,7 +281,8 @@ def tile_multiheadattention_pb_kernel(
         gather_tokens(0)
         turn_bias()
         quantise_tokens(0)
-        project(0)
+        for unit in range(AHEAD):
+            project(unit)
 
         for r in range(UNITS + CHUNKS):
             if r + 1 < GROUPS:
@@ -290,12 +292,12 @@ def tile_multiheadattention_pb_kernel(
                 spread_rows(gain_ps, 0)
             if r == CHUNKS + 1:
                 spread_rows(shift_ps, CHUNKS)
-            if r + 1 < UNITS:
-                project(r + 1)
             if 1 <= r < GROUPS:
                 quantise_tokens(r)
             if r < UNITS:
                 add_residual(r)
+            if r + AHEAD < UNITS:
+                project(r + AHEAD)
             group, step = divmod(r - CHUNKS, CHUNKS)
             if group >= 0:
                 first = group * GROUP_TILES

@@ -21,15 +21,16 @@ BANK = 512
 BANK_BF = 2 * BANK
 CHUNKS = D // BANK
 BLOCKS = BANK // P
+FIRST = 0
+LAST = TILES - 1
 GROUP_TILES = 2
 GROUP = GROUP_TILES * P
-GROUPS = TOKENS // GROUP
+GROUPS = (TILES - 2) // GROUP_TILES
 UNITS = GROUPS * CHUNKS
 LN_EPS = 1e-5
-POOL_COLS = 640
-POOL_COLS_LAST = 384
-POOL_FROM = D - POOL_COLS
-VECTOR_MOST = D - POOL_COLS_LAST
+POOL_MOST = 1024
+POOL_LEAST = 512
+POOL_ALONE = 3
 AHEAD = 2
 
 FLOPS = 2 * TOKENS * K * D
@@ -51,27 +52,25 @@ def tile_multiheadattention_pb_kernel(
         tc.tile_pool(name="stats", bufs=TILES) as stats,
         tc.psum_pool(name="spread", bufs=1) as spread,
         tc.psum_pool(name="by_feature", bufs=2) as by_feature,
-        tc.psum_pool(name="by_token", bufs=2) as by_token,
+        tc.psum_pool(name="by_token", bufs=3) as by_token,
         tc.manual_schedule(),
     ):
         ident = keep.tile([P, P], F32)
         make_identity(nc, ident[:])
+        bias_chunks = keep.tile([P, BANK], BF16)
+        nc.vector.memset(bias_chunks[:].bitcast(I32), 0)
+        w_plane = keep.tile([P, D], U8, align_bytes=64)
+        nc.vector.memset(w_plane[:].bitcast(I32), 0)
         bias_rows = keep.tile([P, P], BF16)
         nc.vector.memset(bias_rows[:].bitcast(I32), 0)
         norm_rows = keep.tile([P, BANK], BF16)
         nc.vector.memset(norm_rows[:].bitcast(I32), 0)
-        w_plane = keep.tile([P, D], U8, align_bytes=64)
-        nc.vector.memset(w_plane[:].bitcast(I32), 0)
         eps = keep.tile([P, 1], F32)
         nc.vector.memset(eps[:], LN_EPS)
         ident_bf = keep.tile([P, P], BF16)
         nc.vector.tensor_copy(out=ident_bf[:], in_=ident[:])
 
         nc.gpsimd.dma_start(out=bias_rows[0 : D // P, :], in_=proj_b.rearrange("(j p) -> j p", p=P))
-        nc.gpsimd.dma_start(out=norm_rows[0:CHUNKS, :], in_=ln_g.rearrange("(c n) -> c n", n=BANK))
-        nc.gpsimd.dma_start(
-            out=norm_rows[CHUNKS : 2 * CHUNKS, :], in_=ln_b.rearrange("(c n) -> c n", n=BANK)
-        )
         warm = keep.tile([P, 1], F32)
         nc.scalar.activation(out=warm[:], in_=eps[:], func=ACT.Abs_reciprocal_sqrt)
 
@@ -84,98 +83,130 @@ def tile_multiheadattention_pb_kernel(
                 out=x_sb[:, i, :].rearrange("p (h j) -> p h j", h=HEADS), in_=x_dram[i]
             )
 
-        def load_words(chunk):
-            cols = slice(chunk * 2 * BANK, (chunk + 1) * 2 * BANK)
+        def load_words(half):
+            cols = slice(half * D, (half + 1) * D)
             nc.sync.dma_start(out=w_words[:, cols].bitcast(I32), in_=proj_w_words[0][:, cols].bitcast(I32))
 
         def load_residual(i):
             nc.sync.dma_start(out=res_sb[:, i, :], in_=res_dram[i])
 
-        for i in range(GROUP_TILES):
-            load_x(i)
-        load_words(0)
+        load_x(FIRST)
+        nc.sync.dma_start(
+            out=bias_chunks[0:CHUNKS, :], in_=proj_b.rearrange("(c n) -> c n", n=BANK)
+        )
+        load_residual(FIRST)
         for quadrant in range(4):
             nc.sync.dma_start(
                 out=w_plane[32 * quadrant : 32 * quadrant + 4, :].bitcast(I32),
                 in_=proj_w_scales[0, 4 * quadrant : 4 * quadrant + 4, :].bitcast(I32),
             )
-        load_residual(0)
+        load_words(0)
         load_words(1)
+        load_x(1)
+        load_x(2)
+        nc.sync.dma_start(out=norm_rows[0:CHUNKS, :], in_=ln_g.rearrange("(c n) -> c n", n=BANK))
+        nc.sync.dma_start(
+            out=norm_rows[CHUNKS : 2 * CHUNKS, :], in_=ln_b.rearrange("(c n) -> c n", n=BANK)
+        )
+        load_residual(LAST)
         load_residual(1)
-        for group in range(1, GROUPS):
-            for i in range(group * GROUP_TILES, (group + 1) * GROUP_TILES):
-                load_x(i)
-            if group + 1 < CHUNKS:
-                load_words(group + 1)
-        for i in range(GROUP_TILES, TILES):
+        load_residual(2)
+        for i in range(3, TILES):
+            load_x(i)
+        for i in range(3, LAST):
             load_residual(i)
-        gain_sb = keep.tile([P, POOL_COLS], BF16)
-        shift_sb = keep.tile([P, POOL_COLS], BF16)
-        nc.sync.dma_start(out=gain_sb[:], in_=ln_g[POOL_FROM:D].partition_broadcast(P))
-        nc.sync.dma_start(out=shift_sb[:], in_=ln_b[POOL_FROM:D].partition_broadcast(P))
 
-        bias_cols = keep.tile([P, D // P], F32)
-
-        def turn_bias():
-            bias_ps = by_feature.tile([P, P], BF16, tag="product")
-            nc.tensor.transpose(bias_ps[:], bias_rows[:], ident_bf[:])
-            nc.scalar.copy(out=bias_cols[:], in_=bias_ps[:, 0 : D // P])
-
-        gain_ps = [spread.tile([P, BANK_BF], BF16, name="gain_ps%d" % h) for h in range(2)]
-        shift_ps = [spread.tile([P, BANK_BF], BF16, name="shift_ps%d" % h) for h in range(2)]
-
-        def spread_rows(banks, first_row):
-            for chunk in range(CHUNKS):
-                row = first_row + chunk
-                half, part = divmod(chunk, 2)
-                width = min(BANK, VECTOR_MOST - chunk * BANK)
-                nc.tensor.matmul(
-                    out=banks[half][:, part * BANK : part * BANK + width],
-                    lhsT=ident_bf[:, row : row + 1].to_broadcast([P, P]),
-                    rhs=norm_rows[:, 0:width],
-                    start=True,
-                    stop=True,
-                )
+        def spread_row(bank, part, rows, row):
+            nc.tensor.matmul(
+                out=bank[:, part * BANK : (part + 1) * BANK],
+                lhsT=ident_bf[:, row : row + 1].to_broadcast([P, P]),
+                rhs=rows[:],
+                start=True,
+                stop=True,
+            )
 
         x_codes = keep.tile([P, TILES * P], U32, align_bytes=64)
         x_plane = keep.tile([P, TILES * P], U8, align_bytes=64)
         grouped = {}
-
         flipped = {}
 
-        def flip_tokens(group):
-            flipped[group] = by_token.tile([P, GROUP_TILES, 2, P], F32, name="flipped", tag="turned")
-            for a in range(GROUP_TILES):
-                x_words = x_sb[:, group * GROUP_TILES + a, :].bitcast(F32)
+        def flip_tokens(tiles):
+            key = tiles[0]
+            flipped[key] = by_token.tile([P, len(tiles), 2, P], F32, name="flipped", tag="turned")
+            for a, i in enumerate(tiles):
+                x_words = x_sb[:, i, :].bitcast(F32)
                 for u in range(2):
-                    nc.tensor.transpose(
-                        flipped[group][:, a, u, :], x_words[:, u : K // 2 : 2], ident[:]
-                    )
+                    nc.tensor.transpose(flipped[key][:, a, u, :], x_words[:, u : K // 2 : 2], ident[:])
 
-        def gather_tokens(group):
-            grouped[group] = stage.tile([P, GROUP * 4], BF16, align_bytes=64, name="grouped")
+        def gather_tokens(tiles):
+            key = tiles[0]
+            grouped[key] = stage.tile([P, len(tiles) * P * 4], BF16, align_bytes=64, name="grouped")
             nc.scalar.copy(
-                out=grouped[group][:].bitcast(F32).rearrange("p (a r u) -> p a r u", a=GROUP_TILES, u=2),
-                in_=flipped[group][:].rearrange("p a u r -> p a r u"),
+                out=grouped[key][:].bitcast(F32).rearrange("p (a r u) -> p a r u", a=len(tiles), u=2),
+                in_=flipped[key][:].rearrange("p a u r -> p a r u"),
             )
 
-        def quantise_tokens(group):
-            tokens = slice(group * GROUP, (group + 1) * GROUP)
+        def quantise_tokens(tiles):
+            key = tiles[0]
+            tokens = slice(key * P, (key + len(tiles)) * P)
             nc.vector.quantize_mx(
-                out=x_codes[:, tokens].bitcast(FP8X4), scales=x_plane[:, tokens], in_=grouped[group][:]
+                out=x_codes[:, tokens].bitcast(FP8X4), scales=x_plane[:, tokens], in_=grouped[key][:]
             )
 
+        def group_tiles(group):
+            return [1 + group * GROUP_TILES + a for a in range(GROUP_TILES)]
+
+        bias_cols = keep.tile([P, D // P], F32)
         biased = {}
         y = {}
         sums = {}
         neg_mean = {}
         rstd = {}
         gained = {}
-        result = {}
+        pooled = {}
+
+        def turn_bias():
+            bias_ps = by_feature.tile([P, P], BF16, tag="product")
+            nc.tensor.transpose(bias_ps[:], bias_rows[:], ident_bf[:])
+            nc.scalar.copy(out=bias_cols[:], in_=bias_ps[:, 0 : D // P])
+
+        def add_chunk(i, chunk, product, addend):
+            cols = slice(chunk * BANK, (chunk + 1) * BANK)
+            if chunk == 0:
+                y[i] = work.tile([P, D], F32, name="y", bufs=6)
+                sums[i] = stats.tile([P, CHUNKS], F32, name="sums")
+            nc.vector.scalar_tensor_tensor(
+                out=y[i][:, cols], in0=product[:], scalar=0.0, in1=addend,
+                op0=ALU.add, op1=ALU.add, accum_out=sums[i][:, chunk : chunk + 1],
+            )
+
+        def find_mean(i):
+            scaled_sums = stats.tile([P, CHUNKS], F32, name="scaled_sums")
+            neg_mean[i] = stats.tile([P, 1], F32, name="neg_mean")
+            nc.scalar.activation(
+                out=scaled_sums[:], in_=sums[i][:], func=ACT.Copy, scale=-1.0 / D,
+                accum_out=neg_mean[i][:],
+            )
+
+        def direct(i, chunk, with_bias):
+            cols = slice(chunk * BANK, (chunk + 1) * BANK)
+            tokens = slice(i * P, (i + 1) * P)
+            product = by_token.tile([P, BANK], F32, name="direct_product", tag="turned")
+            nc.tensor.matmul_mx(
+                out=product[:],
+                lhsT=x_codes[:, tokens].bitcast(FP8X4),
+                lhsT_scale=x_plane[:, tokens],
+                rhs=w_words[:, 2 * chunk * BANK : 2 * (chunk + 1) * BANK].bitcast(FP4X4),
+                rhs_scale=w_plane[:, cols],
+                start=True,
+                stop=True,
+            )
+            add_chunk(i, chunk, product, with_bias[:, cols])
 
         def project(unit):
             group, chunk = divmod(unit, CHUNKS)
-            tokens = slice(group * GROUP, (group + 1) * GROUP)
+            first = group_tiles(group)[0]
+            tokens = slice(first * P, first * P + GROUP)
             biased[unit] = work.tile([P, BLOCKS, GROUP], F32, name="biased", bufs=AHEAD + 2)
             for pair in range(BLOCKS // 2):
                 product = by_feature.tile([P, 2, GROUP], F32, tag="product")
@@ -199,48 +230,39 @@ def tile_multiheadattention_pb_kernel(
 
         def add_residual(unit):
             group, chunk = divmod(unit, CHUNKS)
-            cols = slice(chunk * BANK, (chunk + 1) * BANK)
-            for a in range(GROUP_TILES):
-                i = group * GROUP_TILES + a
-                if chunk == 0:
-                    y[i] = work.tile([P, D], F32, name="y", bufs=TILES)
-                    sums[i] = stats.tile([P, CHUNKS], F32, name="sums")
+            for a, i in enumerate(group_tiles(group)):
                 turned = by_token.tile([P, BANK], F32, tag="turned")
                 for b in range(BLOCKS):
                     nc.tensor.transpose(
                         turned[:, b * P : (b + 1) * P], biased[unit][:, b, a * P : (a + 1) * P], ident[:]
                     )
-                nc.vector.scalar_tensor_tensor(
-                    out=y[i][:, cols],
-                    in0=turned[:],
-                    scalar=0.0,
-                    in1=res_sb[:, i, cols],
-                    op0=ALU.add,
-                    op1=ALU.add,
-                    accum_out=sums[i][:, chunk : chunk + 1],
-                )
+                add_chunk(i, chunk, turned, res_sb[:, i, chunk * BANK : (chunk + 1) * BANK])
                 if chunk == CHUNKS - 1:
-                    scaled_sums = stats.tile([P, CHUNKS], F32, name="scaled_sums")
-                    neg_mean[i] = stats.tile([P, 1], F32, name="neg_mean")
-                    nc.scalar.activation(
-                        out=scaled_sums[:], in_=sums[i][:], func=ACT.Copy, scale=-1.0 / D,
-                        accum_out=neg_mean[i][:],
-                    )
+                    find_mean(i)
 
-        def pool_from(i):
-            return D - (POOL_COLS_LAST if i // GROUP_TILES == GROUPS - 1 else POOL_COLS)
+        gain_lo = []
+        shift_lo = []
+        middle = []
+        pool_rows = keep.tile([P, 2, D - BANK_BF], BF16)
+
+        def pool_cols(i):
+            return POOL_LEAST if i >= TILES - 3 else POOL_MOST
 
         def vector_parts(i):
-            end = pool_from(i)
-            return [(lo, min(lo + BANK_BF, end)) for lo in range(0, end, BANK_BF)]
+            parts = [(0, BANK_BF, gain_lo[0][:], shift_lo[0][:])]
+            width = D - pool_cols(i) - BANK_BF
+            if width > 0:
+                parts.append(
+                    (BANK_BF, BANK_BF + width, middle[0][:, 0:width], middle[0][:, BANK : BANK + width])
+                )
+            return parts
 
         def centre_and_gain(i):
-            gained[i] = work.tile([P, D], F32, name="gained")
-            for lo, hi in vector_parts(i):
+            gained[i] = work.tile([P, D - POOL_LEAST], F32, name="gained")
+            for lo, hi, gain, shift in vector_parts(i):
                 nc.vector.scalar_tensor_tensor(
                     out=gained[i][:, lo:hi], in0=y[i][:, lo:hi], scalar=neg_mean[i][:],
-                    in1=gain_ps[lo // BANK_BF][:, 0 : hi - lo],
-                    op0=ALU.add, op1=ALU.mult,
+                    in1=gain, op0=ALU.add, op1=ALU.mult,
                 )
 
         def deviation(i):
@@ -256,60 +278,136 @@ def tile_multiheadattention_pb_kernel(
             )
 
         def pool_columns(i):
-            result[i] = work.tile([P, D], F32, name="result", bufs=4)
-            first = pool_from(i)
-            mine = result[i][:, first:D]
-            nc.gpsimd.tensor_scalar(
-                out=mine, in0=y[i][:, first:D], scalar1=neg_mean[i][:], scalar2=rstd[i][:],
-                op0=ALU.add, op1=ALU.mult,
-            )
-            nc.gpsimd.tensor_tensor(out=mine, in0=mine, in1=gain_sb[:, first - POOL_FROM :], op=ALU.mult)
-            nc.gpsimd.tensor_tensor(out=mine, in0=mine, in1=shift_sb[:, first - POOL_FROM :], op=ALU.add)
+            pooled[i] = work.tile([P, POOL_MOST], F32, name="pooled", bufs=5)
+            first = D - pool_cols(i)
+            mine = pooled[i][:, 0 : pool_cols(i)]
+            if i < POOL_ALONE:
+                nc.gpsimd.tensor_scalar(
+                    out=mine, in0=y[i][:, first:D], scalar1=neg_mean[i][:], scalar2=rstd[i][:],
+                    op0=ALU.add, op1=ALU.mult,
+                )
+            else:
+                offset = stats.tile([P, 1], F32, name="offset")
+                nc.scalar.activation(out=offset[:], in_=neg_mean[i][:], func=ACT.Copy, scale=rstd[i][:])
+                nc.scalar.activation(
+                    out=mine, in_=y[i][:, first:D], func=ACT.Identity, bias=offset[:], scale=rstd[i][:]
+                )
+            gain = pool_rows[:, 0, first - BANK_BF :]
+            shift = pool_rows[:, 1, first - BANK_BF :]
+            nc.gpsimd.tensor_tensor(out=mine, in0=mine, in1=gain, op=ALU.mult)
+            nc.gpsimd.tensor_tensor(out=mine, in0=mine, in1=shift, op=ALU.add)
 
         def scale_shift_store(i):
-            for lo, hi in vector_parts(i):
+            result = work.tile([P, D - POOL_LEAST], F32, name="result")
+            for lo, hi, gain, shift in vector_parts(i):
                 nc.vector.scalar_tensor_tensor(
-                    out=result[i][:, lo:hi], in0=gained[i][:, lo:hi], scalar=rstd[i][:],
-                    in1=shift_ps[lo // BANK_BF][:, 0 : hi - lo],
-                    op0=ALU.mult, op1=ALU.add,
+                    out=result[:, lo:hi], in0=gained[i][:, lo:hi], scalar=rstd[i][:],
+                    in1=shift, op0=ALU.mult, op1=ALU.add,
                 )
-                nc.sync.dma_start(out=out_dram[i][:, lo:hi], in_=result[i][:, lo:hi])
-            first = pool_from(i)
-            nc.sync.dma_start(out=out_dram[i][:, first:D], in_=result[i][:, first:D])
+                nc.sync.dma_start(out=out_dram[i][:, lo:hi], in_=result[:, lo:hi])
 
-        flip_tokens(0)
-        gather_tokens(0)
+        def store_pooled(i):
+            nc.sync.dma_start(out=out_dram[i][:, D - pool_cols(i) : D], in_=pooled[i][:, 0 : pool_cols(i)])
+
+        def norm_first(i):
+            centre_and_gain(i)
+            deviation(i)
+            pool_columns(i)
+
+        first_addend = keep.tile([P, D], F32)
+        last_addend = keep.tile([P, D], F32)
+        bias_sb = keep.tile([P, D], BF16)
+        bias_ps = [spread.tile([P, BANK_BF], BF16, name="bias_ps%d" % h, tag="lo%d" % h) for h in range(2)]
+
+        def add_bias_first(half):
+            cols = slice(half * BANK_BF, (half + 1) * BANK_BF)
+            nc.vector.tensor_tensor(
+                out=first_addend[:, cols], in0=res_sb[:, FIRST, cols], in1=bias_ps[half][:], op=ALU.add
+            )
+
+        def keep_bias(half):
+            nc.scalar.copy(out=bias_sb[:, half * BANK_BF : (half + 1) * BANK_BF], in_=bias_ps[half][:])
+
+        flip_tokens([FIRST])
+        gather_tokens([FIRST])
+        for chunk in range(CHUNKS):
+            spread_row(bias_ps[chunk // 2], chunk % 2, bias_chunks, chunk)
+        add_bias_first(0)
+        quantise_tokens([FIRST])
+        keep_bias(0)
+        add_bias_first(1)
+        direct(FIRST, 0, first_addend)
+        direct(FIRST, 1, first_addend)
+        flip_tokens(group_tiles(0))
+        gather_tokens(group_tiles(0))
         turn_bias()
-        quantise_tokens(0)
-        for unit in range(AHEAD):
-            project(unit)
+        keep_bias(1)
+        quantise_tokens(group_tiles(0))
+        direct(FIRST, 2, first_addend)
+        direct(FIRST, 3, first_addend)
+        project(0)
+        gain_lo.append(spread.tile([P, BANK_BF], BF16, name="gain_lo", tag="lo0"))
+        shift_lo.append(spread.tile([P, BANK_BF], BF16, name="shift_lo", tag="lo1"))
+        middle.append(spread.tile([P, BANK_BF], BF16, name="middle"))
+        for chunk in range(2):
+            spread_row(gain_lo[0], chunk, norm_rows, chunk)
+        for quarter in range(4):
+            cols = slice(quarter * BANK, (quarter + 1) * BANK)
+            nc.gpsimd.tensor_tensor(
+                out=last_addend[:, cols], in0=res_sb[:, LAST, cols], in1=bias_sb[:, cols], op=ALU.add
+            )
+        find_mean(FIRST)
+        centre_and_gain(FIRST)
+        deviation(FIRST)
+        project(1)
+        for chunk in range(2):
+            spread_row(shift_lo[0], chunk, norm_rows, CHUNKS + chunk)
+        top = by_token.tile([P, BANK_BF], BF16, name="top", tag="turned")
+        for half, bank in enumerate([middle[0], top]):
+            for vector in range(2):
+                spread_row(bank, vector, norm_rows, vector * CHUNKS + 2 + half)
+        for half, bank in enumerate([middle[0], top]):
+            nc.vector.tensor_copy(
+                out=pool_rows[:, :, half * BANK : (half + 1) * BANK],
+                in_=bank[:].rearrange("p (v n) -> p v n", n=BANK),
+            )
+        pool_columns(FIRST)
 
-        for r in range(UNITS + CHUNKS):
-            if r + 1 < GROUPS:
-                flip_tokens(r + 1)
-                gather_tokens(r + 1)
-            if r == CHUNKS:
-                spread_rows(gain_ps, 0)
-            if r == CHUNKS + 1:
-                spread_rows(shift_ps, CHUNKS)
-            if 1 <= r < GROUPS:
-                quantise_tokens(r)
+        later = [group_tiles(1), group_tiles(2), [LAST]]
+        for r in range(UNITS + 5):
+            if r < len(later):
+                flip_tokens(later[r])
+                gather_tokens(later[r])
             if r < UNITS:
                 add_residual(r)
+            if r < len(later):
+                quantise_tokens(later[r])
             if r + AHEAD < UNITS:
                 project(r + AHEAD)
+            if r in (UNITS, UNITS + 1):
+                for chunk in range(2):
+                    direct(LAST, 2 * (r - UNITS) + chunk, last_addend)
+            if r == UNITS + 1:
+                find_mean(LAST)
+            if r == 0:
+                scale_shift_store(FIRST)
+            if r == 3:
+                store_pooled(FIRST)
             group, step = divmod(r - CHUNKS, CHUNKS)
-            if group >= 0:
-                first = group * GROUP_TILES
+            if 0 <= group < GROUPS:
+                first, second = group_tiles(group)
                 if step == 0:
-                    centre_and_gain(first)
-                    deviation(first)
+                    norm_first(first)
                 if step == 1:
-                    centre_and_gain(first + 1)
-                    deviation(first + 1)
-                    pool_columns(first)
+                    norm_first(second)
                 if step == 2:
-                    pool_columns(first + 1)
                     scale_shift_store(first)
+                    store_pooled(first)
+                    if r == UNITS + 2:
+                        norm_first(LAST)
                 if step == 3:
-                    scale_shift_store(first + 1)
+                    scale_shift_store(second)
+                    store_pooled(second)
+            if r == UNITS + 4:
+                scale_shift_store(LAST)
+                store_pooled(LAST)

@@ -108,12 +108,10 @@ def tile_multiheadattention_pb_kernel(
         nc.sync.dma_start(
             out=norm_rows[CHUNKS : 2 * CHUNKS, :], in_=ln_b.rearrange("(c n) -> c n", n=BANK)
         )
-        load_residual(LAST)
-        load_residual(1)
-        load_residual(2)
         for i in range(3, TILES):
             load_x(i)
-        for i in range(3, LAST):
+        load_residual(LAST)
+        for i in range(1, LAST):
             load_residual(i)
 
         def spread_row(bank, part, rows, row):
@@ -346,6 +344,10 @@ def tile_multiheadattention_pb_kernel(
         direct(FIRST, 2, first_addend)
         direct(FIRST, 3, first_addend)
         project(0)
+        for tiles in (group_tiles(1), group_tiles(2), [LAST]):
+            flip_tokens(tiles)
+            gather_tokens(tiles)
+            quantise_tokens(tiles)
         gain_lo.append(spread.tile([P, BANK_BF], BF16, name="gain_lo", tag="lo0"))
         shift_lo.append(spread.tile([P, BANK_BF], BF16, name="shift_lo", tag="lo1"))
         middle.append(spread.tile([P, BANK_BF], BF16, name="middle"))
@@ -373,15 +375,9 @@ def tile_multiheadattention_pb_kernel(
             )
         pool_columns(FIRST)
 
-        later = [group_tiles(1), group_tiles(2), [LAST]]
         for r in range(UNITS + 5):
-            if r < len(later):
-                flip_tokens(later[r])
-                gather_tokens(later[r])
             if r < UNITS:
                 add_residual(r)
-            if r < len(later):
-                quantise_tokens(later[r])
             if r + AHEAD < UNITS:
                 project(r + AHEAD)
             if r in (UNITS, UNITS + 1):

@@ -353,11 +353,6 @@ def tile_multiheadattention_pb_kernel(
         middle.append(spread.tile([P, BANK_BF], BF16, name="middle"))
         for chunk in range(2):
             spread_row(gain_lo[0], chunk, norm_rows, chunk)
-        for quarter in range(4):
-            cols = slice(quarter * BANK, (quarter + 1) * BANK)
-            nc.gpsimd.tensor_tensor(
-                out=last_addend[:, cols], in0=res_sb[:, LAST, cols], in1=bias_sb[:, cols], op=ALU.add
-            )
         find_mean(FIRST)
         centre_and_gain(FIRST)
         deviation(FIRST)
@@ -374,6 +369,11 @@ def tile_multiheadattention_pb_kernel(
                 in_=bank[:].rearrange("p (v n) -> p v n", n=BANK),
             )
         pool_columns(FIRST)
+        for quarter in range(4):
+            cols = slice(quarter * BANK, (quarter + 1) * BANK)
+            nc.gpsimd.tensor_tensor(
+                out=last_addend[:, cols], in0=res_sb[:, LAST, cols], in1=bias_sb[:, cols], op=ALU.add
+            )
 
         for r in range(UNITS + 5):
             if r < UNITS:

@@ -21,16 +21,15 @@ BANK = 512
 BANK_BF = 2 * BANK
 CHUNKS = D // BANK
 BLOCKS = BANK // P
-FIRST = 0
-LAST = TILES - 1
+FIRST, SECOND = 0, 1
 GROUP_TILES = 2
 GROUP = GROUP_TILES * P
 GROUPS = (TILES - 2) // GROUP_TILES
 UNITS = GROUPS * CHUNKS
 LN_EPS = 1e-5
-POOL_MOST = 1024
-POOL_LEAST = 512
-POOL_ALONE = 3
+POOL_COLS = (1024, 896, 640, 512)
+POOL_ALONE = 6
+BIAS_LATE = 4
 AHEAD = 2
 
 FLOPS = 2 * TOKENS * K * D
@@ -87,31 +86,36 @@ def tile_multiheadattention_pb_kernel(
             cols = slice(half * D, (half + 1) * D)
             nc.sync.dma_start(out=w_words[:, cols].bitcast(I32), in_=proj_w_words[0][:, cols].bitcast(I32))
 
-        def load_residual(i):
-            nc.sync.dma_start(out=res_sb[:, i, :], in_=res_dram[i])
+        def load_residual(i, lo=0, hi=D):
+            nc.sync.dma_start(out=res_sb[:, i, lo:hi], in_=res_dram[i][:, lo:hi])
+
+        def load_scales():
+            for quadrant in range(4):
+                nc.sync.dma_start(
+                    out=w_plane[32 * quadrant : 32 * quadrant + 4, :].bitcast(I32),
+                    in_=proj_w_scales[0, 4 * quadrant : 4 * quadrant + 4, :].bitcast(I32),
+                )
 
         load_x(FIRST)
         nc.sync.dma_start(
             out=bias_chunks[0:CHUNKS, :], in_=proj_b.rearrange("(c n) -> c n", n=BANK)
         )
-        load_residual(FIRST)
-        for quadrant in range(4):
-            nc.sync.dma_start(
-                out=w_plane[32 * quadrant : 32 * quadrant + 4, :].bitcast(I32),
-                in_=proj_w_scales[0, 4 * quadrant : 4 * quadrant + 4, :].bitcast(I32),
-            )
-        load_words(0)
-        load_words(1)
-        load_x(1)
         load_x(2)
+        load_x(3)
+        load_residual(FIRST, 0, BANK_BF)
+        load_scales()
+        load_words(0)
+        load_residual(FIRST, BANK_BF, D)
+        load_words(1)
         nc.sync.dma_start(out=norm_rows[0:CHUNKS, :], in_=ln_g.rearrange("(c n) -> c n", n=BANK))
         nc.sync.dma_start(
             out=norm_rows[CHUNKS : 2 * CHUNKS, :], in_=ln_b.rearrange("(c n) -> c n", n=BANK)
         )
-        for i in range(3, TILES):
+        load_x(SECOND)
+        load_residual(SECOND)
+        for i in range(4, TILES):
             load_x(i)
-        load_residual(LAST)
-        for i in range(1, LAST):
+        for i in range(2, TILES):
             load_residual(i)
 
         def spread_row(bank, part, rows, row):
@@ -152,7 +156,7 @@ def tile_multiheadattention_pb_kernel(
             )
 
         def group_tiles(group):
-            return [1 + group * GROUP_TILES + a for a in range(GROUP_TILES)]
+            return [2 + group * GROUP_TILES + a for a in range(GROUP_TILES)]
 
         bias_cols = keep.tile([P, D // P], F32)
         biased = {}
@@ -219,6 +223,9 @@ def tile_multiheadattention_pb_kernel(
                         start=True,
                         stop=True,
                     )
+                if unit >= BIAS_LATE:
+                    nc.scalar.copy(out=biased[unit][:, 2 * pair : 2 * pair + 2, :], in_=product[:])
+                    continue
                 for e in range(2):
                     j = chunk * BLOCKS + 2 * pair + e
                     nc.scalar.activation(
@@ -230,9 +237,25 @@ def tile_multiheadattention_pb_kernel(
             group, chunk = divmod(unit, CHUNKS)
             for a, i in enumerate(group_tiles(group)):
                 turned = by_token.tile([P, BANK], F32, tag="turned")
+                if unit >= BIAS_LATE:
+                    for b in range(BLOCKS):
+                        j = chunk * BLOCKS + b
+                        nc.tensor.matmul(
+                            out=turned[:, b * P : (b + 1) * P],
+                            lhsT=bias_cols[:, j : j + 1].to_broadcast([P, P]),
+                            rhs=ident[:],
+                            is_transpose=True,
+                            start=(b == 0),
+                            stop=False,
+                        )
                 for b in range(BLOCKS):
-                    nc.tensor.transpose(
-                        turned[:, b * P : (b + 1) * P], biased[unit][:, b, a * P : (a + 1) * P], ident[:]
+                    nc.tensor.matmul(
+                        out=turned[:, b * P : (b + 1) * P],
+                        lhsT=biased[unit][:, b, a * P : (a + 1) * P],
+                        rhs=ident[:],
+                        is_transpose=True,
+                        start=(b == 0 and unit < BIAS_LATE),
+                        stop=(b == BLOCKS - 1),
                     )
                 add_chunk(i, chunk, turned, res_sb[:, i, chunk * BANK : (chunk + 1) * BANK])
                 if chunk == CHUNKS - 1:
@@ -244,7 +267,7 @@ def tile_multiheadattention_pb_kernel(
         pool_rows = keep.tile([P, 2, D - BANK_BF], BF16)
 
         def pool_cols(i):
-            return POOL_LEAST if i >= TILES - 3 else POOL_MOST
+            return POOL_COLS[i // 2]
 
         def vector_parts(i):
             parts = [(0, BANK_BF, gain_lo[0][:], shift_lo[0][:])]
@@ -256,7 +279,7 @@ def tile_multiheadattention_pb_kernel(
             return parts
 
         def centre_and_gain(i):
-            gained[i] = work.tile([P, D - POOL_LEAST], F32, name="gained")
+            gained[i] = work.tile([P, D - POOL_COLS[3]], F32, name="gained")
             for lo, hi, gain, shift in vector_parts(i):
                 nc.vector.scalar_tensor_tensor(
                     out=gained[i][:, lo:hi], in0=y[i][:, lo:hi], scalar=neg_mean[i][:],
@@ -276,7 +299,7 @@ def tile_multiheadattention_pb_kernel(
             )
 
         def pool_columns(i):
-            pooled[i] = work.tile([P, POOL_MOST], F32, name="pooled", bufs=5)
+            pooled[i] = work.tile([P, POOL_COLS[0]], F32, name="pooled", bufs=5)
             first = D - pool_cols(i)
             mine = pooled[i][:, 0 : pool_cols(i)]
             if i < POOL_ALONE:
@@ -296,7 +319,7 @@ def tile_multiheadattention_pb_kernel(
             nc.gpsimd.tensor_tensor(out=mine, in0=mine, in1=shift, op=ALU.add)
 
         def scale_shift_store(i):
-            result = work.tile([P, D - POOL_LEAST], F32, name="result")
+            result = work.tile([P, D - POOL_COLS[3]], F32, name="result")
             for lo, hi, gain, shift in vector_parts(i):
                 nc.vector.scalar_tensor_tensor(
                     out=result[:, lo:hi], in0=gained[i][:, lo:hi], scalar=rstd[i][:],
@@ -313,7 +336,7 @@ def tile_multiheadattention_pb_kernel(
             pool_columns(i)
 
         first_addend = keep.tile([P, D], F32)
-        last_addend = keep.tile([P, D], F32)
+        second_addend = keep.tile([P, D], F32)
         bias_sb = keep.tile([P, D], BF16)
         bias_ps = [spread.tile([P, BANK_BF], BF16, name="bias_ps%d" % h, tag="lo%d" % h) for h in range(2)]
 
@@ -330,21 +353,22 @@ def tile_multiheadattention_pb_kernel(
         gather_tokens([FIRST])
         for chunk in range(CHUNKS):
             spread_row(bias_ps[chunk // 2], chunk % 2, bias_chunks, chunk)
-        add_bias_first(0)
-        quantise_tokens([FIRST])
-        keep_bias(0)
-        add_bias_first(1)
-        direct(FIRST, 0, first_addend)
-        direct(FIRST, 1, first_addend)
         flip_tokens(group_tiles(0))
         gather_tokens(group_tiles(0))
         turn_bias()
-        keep_bias(1)
+        quantise_tokens([FIRST])
+        add_bias_first(0)
         quantise_tokens(group_tiles(0))
+        add_bias_first(1)
+        project(0)
+        direct(FIRST, 0, first_addend)
+        direct(FIRST, 1, first_addend)
+        project(1)
+        keep_bias(0)
+        keep_bias(1)
         direct(FIRST, 2, first_addend)
         direct(FIRST, 3, first_addend)
-        project(0)
-        for tiles in (group_tiles(1), group_tiles(2), [LAST]):
+        for tiles in ([SECOND], group_tiles(1), group_tiles(2)):
             flip_tokens(tiles)
             gather_tokens(tiles)
             quantise_tokens(tiles)
@@ -353,10 +377,17 @@ def tile_multiheadattention_pb_kernel(
         middle.append(spread.tile([P, BANK_BF], BF16, name="middle"))
         for chunk in range(2):
             spread_row(gain_lo[0], chunk, norm_rows, chunk)
+        for part in range(8):
+            cols = slice(part * D // 8, (part + 1) * D // 8)
+            nc.gpsimd.tensor_tensor(
+                out=second_addend[:, cols], in0=res_sb[:, SECOND, cols], in1=bias_sb[:, cols], op=ALU.add
+            )
         find_mean(FIRST)
-        centre_and_gain(FIRST)
         deviation(FIRST)
-        project(1)
+        add_residual(0)
+        centre_and_gain(FIRST)
+        for unit in range(2, AHEAD):
+            project(unit)
         for chunk in range(2):
             spread_row(shift_lo[0], chunk, norm_rows, CHUNKS + chunk)
         top = by_token.tile([P, BANK_BF], BF16, name="top", tag="turned")
@@ -364,31 +395,30 @@ def tile_multiheadattention_pb_kernel(
             for vector in range(2):
                 spread_row(bank, vector, norm_rows, vector * CHUNKS + 2 + half)
         for half, bank in enumerate([middle[0], top]):
-            nc.vector.tensor_copy(
+            nc.scalar.copy(
                 out=pool_rows[:, :, half * BANK : (half + 1) * BANK],
                 in_=bank[:].rearrange("p (v n) -> p v n", n=BANK),
             )
         pool_columns(FIRST)
-        for quarter in range(4):
-            cols = slice(quarter * BANK, (quarter + 1) * BANK)
-            nc.gpsimd.tensor_tensor(
-                out=last_addend[:, cols], in0=res_sb[:, LAST, cols], in1=bias_sb[:, cols], op=ALU.add
-            )
+        for unit in range(AHEAD, AHEAD + 1):
+            project(unit)
+        for chunk in range(CHUNKS):
+            direct(SECOND, chunk, second_addend)
+        scale_shift_store(FIRST)
 
-        for r in range(UNITS + 5):
+        for r in range(1, UNITS + 4):
             if r < UNITS:
                 add_residual(r)
             if r + AHEAD < UNITS:
                 project(r + AHEAD)
-            if r in (UNITS, UNITS + 1):
-                for chunk in range(2):
-                    direct(LAST, 2 * (r - UNITS) + chunk, last_addend)
-            if r == UNITS + 1:
-                find_mean(LAST)
-            if r == 0:
-                scale_shift_store(FIRST)
-            if r == 3:
+            if r == 1:
+                find_mean(SECOND)
+                norm_first(SECOND)
                 store_pooled(FIRST)
+            if r == 2:
+                scale_shift_store(SECOND)
+            if r == 3:
+                store_pooled(SECOND)
             group, step = divmod(r - CHUNKS, CHUNKS)
             if 0 <= group < GROUPS:
                 first, second = group_tiles(group)
@@ -399,11 +429,6 @@ def tile_multiheadattention_pb_kernel(
                 if step == 2:
                     scale_shift_store(first)
                     store_pooled(first)
-                    if r == UNITS + 2:
-                        norm_first(LAST)
                 if step == 3:
                     scale_shift_store(second)
                     store_pooled(second)
-            if r == UNITS + 4:
-                scale_shift_store(LAST)
-                store_pooled(LAST)

@@ -29,7 +29,7 @@ UNITS = GROUPS * CHUNKS
 LN_EPS = 1e-5
 POOL_COLS = (1024, 896, 640, 512)
 POOL_ALONE = 6
-BIAS_LATE = 4
+BIAS_LATE = 12
 AHEAD = 2
 
 FLOPS = 2 * TOKENS * K * D

@@ -29,7 +29,6 @@ UNITS = GROUPS * CHUNKS
 LN_EPS = 1e-5
 POOL_COLS = (1024, 896, 640, 512)
 POOL_ALONE = 6
-BIAS_LATE = 12
 AHEAD = 2
 
 FLOPS = 2 * TOKENS * K * D
@@ -129,7 +128,7 @@ def tile_multiheadattention_pb_kernel(
 
         x_codes = keep.tile([P, TILES * P], U32, align_bytes=64)
         x_plane = keep.tile([P, TILES * P], U8, align_bytes=64)
-        grouped = {}
+        x_turned = keep.tile([P, TILES * 4 * P], BF16, align_bytes=64)
         flipped = {}
 
         def flip_tokens(tiles):
@@ -140,11 +139,11 @@ def tile_multiheadattention_pb_kernel(
                 for u in range(2):
                     nc.tensor.transpose(flipped[key][:, a, u, :], x_words[:, u : K // 2 : 2], ident[:])
 
-        def gather_tokens(tiles):
+        def gather_tokens(tiles, by_scalar=True):
             key = tiles[0]
-            grouped[key] = stage.tile([P, len(tiles) * P * 4], BF16, align_bytes=64, name="grouped")
-            nc.scalar.copy(
-                out=grouped[key][:].bitcast(F32).rearrange("p (a r u) -> p a r u", a=len(tiles), u=2),
+            copy = nc.scalar.copy if by_scalar else nc.vector.tensor_copy
+            copy(
+                out=x_turned[:, key * 4 * P : (key + len(tiles)) * 4 * P].bitcast(F32).rearrange("p (a r u) -> p a r u", a=len(tiles), u=2),
                 in_=flipped[key][:].rearrange("p a u r -> p a r u"),
             )
 
@@ -152,7 +151,7 @@ def tile_multiheadattention_pb_kernel(
             key = tiles[0]
             tokens = slice(key * P, (key + len(tiles)) * P)
             nc.vector.quantize_mx(
-                out=x_codes[:, tokens].bitcast(FP8X4), scales=x_plane[:, tokens], in_=grouped[key][:]
+                out=x_codes[:, tokens].bitcast(FP8X4), scales=x_plane[:, tokens], in_=x_turned[:, key * 4 * P : (key + len(tiles)) * 4 * P],
             )
 
         def group_tiles(group):
@@ -223,9 +222,6 @@ def tile_multiheadattention_pb_kernel(
                         start=True,
                         stop=True,
                     )
-                if unit >= BIAS_LATE:
-                    nc.scalar.copy(out=biased[unit][:, 2 * pair : 2 * pair + 2, :], in_=product[:])
-                    continue
                 for e in range(2):
                     j = chunk * BLOCKS + 2 * pair + e
                     nc.scalar.activation(
@@ -237,29 +233,11 @@ def tile_multiheadattention_pb_kernel(
             group, chunk = divmod(unit, CHUNKS)
             for a, i in enumerate(group_tiles(group)):
                 turned = by_token.tile([P, BANK], F32, tag="turned")
-                if unit >= BIAS_LATE:
-                    for b in range(BLOCKS):
-                        j = chunk * BLOCKS + b
-                        nc.tensor.matmul(
-                            out=turned[:, b * P : (b + 1) * P],
-                            lhsT=bias_cols[:, j : j + 1].to_broadcast([P, P]),
-                            rhs=ident[:],
-                            is_transpose=True,
-                            start=(b == 0),
-                            stop=False,
-                        )
                 for b in range(BLOCKS):
-                    nc.tensor.matmul(
-                        out=turned[:, b * P : (b + 1) * P],
-                        lhsT=biased[unit][:, b, a * P : (a + 1) * P],
-                        rhs=ident[:],
-                        is_transpose=True,
-                        start=(b == 0 and unit < BIAS_LATE),
-                        stop=(b == BLOCKS - 1),
+                    nc.tensor.transpose(
+                        turned[:, b * P : (b + 1) * P], biased[unit][:, b, a * P : (a + 1) * P], ident[:]
                     )
                 add_chunk(i, chunk, turned, res_sb[:, i, chunk * BANK : (chunk + 1) * BANK])
-                if chunk == CHUNKS - 1:
-                    find_mean(i)
 
         gain_lo = []
         shift_lo = []
@@ -279,7 +257,7 @@ def tile_multiheadattention_pb_kernel(
             return parts
 
         def centre_and_gain(i):
-            gained[i] = work.tile([P, D - POOL_COLS[3]], F32, name="gained")
+            gained[i] = work.tile([P, D], F32, name="gained")
             for lo, hi, gain, shift in vector_parts(i):
                 nc.vector.scalar_tensor_tensor(
                     out=gained[i][:, lo:hi], in0=y[i][:, lo:hi], scalar=neg_mean[i][:],
@@ -299,7 +277,7 @@ def tile_multiheadattention_pb_kernel(
             )
 
         def pool_columns(i):
-            pooled[i] = work.tile([P, POOL_COLS[0]], F32, name="pooled", bufs=5)
+            pooled[i] = work.tile([P, 1024], F32, name="pooled", bufs=5)
             first = D - pool_cols(i)
             mine = pooled[i][:, 0 : pool_cols(i)]
             if i < POOL_ALONE:
@@ -319,7 +297,7 @@ def tile_multiheadattention_pb_kernel(
             nc.gpsimd.tensor_tensor(out=mine, in0=mine, in1=shift, op=ALU.add)
 
         def scale_shift_store(i):
-            result = work.tile([P, D - POOL_COLS[3]], F32, name="result")
+            result = work.tile([P, D], F32, name="result")
             for lo, hi, gain, shift in vector_parts(i):
                 nc.vector.scalar_tensor_tensor(
                     out=result[:, lo:hi], in0=gained[i][:, lo:hi], scalar=rstd[i][:],
@@ -358,20 +336,23 @@ def tile_multiheadattention_pb_kernel(
         turn_bias()
         quantise_tokens([FIRST])
         add_bias_first(0)
+        keep_bias(0)
         quantise_tokens(group_tiles(0))
         add_bias_first(1)
         project(0)
+        keep_bias(1)
         direct(FIRST, 0, first_addend)
         direct(FIRST, 1, first_addend)
         project(1)
-        keep_bias(0)
-        keep_bias(1)
         direct(FIRST, 2, first_addend)
         direct(FIRST, 3, first_addend)
         for tiles in ([SECOND], group_tiles(1), group_tiles(2)):
             flip_tokens(tiles)
-            gather_tokens(tiles)
-            quantise_tokens(tiles)
+        gather_tokens([SECOND], False)
+        gather_tokens(group_tiles(1), False)
+        gather_tokens(group_tiles(2), True)
+        quantise_tokens([SECOND])
+        quantise_tokens(group_tiles(1) + group_tiles(2))
         gain_lo.append(spread.tile([P, BANK_BF], BF16, name="gain_lo", tag="lo0"))
         shift_lo.append(spread.tile([P, BANK_BF], BF16, name="shift_lo", tag="lo1"))
         middle.append(spread.tile([P, BANK_BF], BF16, name="middle"))
@@ -411,6 +392,9 @@ def tile_multiheadattention_pb_kernel(
                 add_residual(r)
             if r + AHEAD < UNITS:
                 project(r + AHEAD)
+            if r < UNITS and r % CHUNKS == CHUNKS - 1:
+                for i in group_tiles(r // CHUNKS):
+                    find_mean(i)
             if r == 1:
                 find_mean(SECOND)
                 norm_first(SECOND)

@@ -27,8 +27,8 @@ GROUP = GROUP_TILES * P
 GROUPS = (TILES - 2) // GROUP_TILES
 UNITS = GROUPS * CHUNKS
 LN_EPS = 1e-5
-POOL_COLS = (1024, 896, 640, 512)
-POOL_ALONE = 6
+POOL_COLS = (1024, 896, 768, 512)
+POOL_ALONE = 5
 AHEAD = 2
 
 FLOPS = 2 * TOKENS * K * D
@@ -257,7 +257,7 @@ def tile_multiheadattention_pb_kernel(
             return parts
 
         def centre_and_gain(i):
-            gained[i] = work.tile([P, D], F32, name="gained")
+            gained[i] = work.tile([P, D - POOL_COLS[3]], F32, name="gained")
             for lo, hi, gain, shift in vector_parts(i):
                 nc.vector.scalar_tensor_tensor(
                     out=gained[i][:, lo:hi], in0=y[i][:, lo:hi], scalar=neg_mean[i][:],
@@ -277,7 +277,7 @@ def tile_multiheadattention_pb_kernel(
             )
 
         def pool_columns(i):
-            pooled[i] = work.tile([P, 1024], F32, name="pooled", bufs=5)
+            pooled[i] = work.tile([P, POOL_COLS[0]], F32, name="pooled", bufs=5)
             first = D - pool_cols(i)
             mine = pooled[i][:, 0 : pool_cols(i)]
             if i < POOL_ALONE:
@@ -297,7 +297,7 @@ def tile_multiheadattention_pb_kernel(
             nc.gpsimd.tensor_tensor(out=mine, in0=mine, in1=shift, op=ALU.add)
 
         def scale_shift_store(i):
-            result = work.tile([P, D], F32, name="result")
+            result = work.tile([P, D - POOL_COLS[3]], F32, name="result")
             for lo, hi, gain, shift in vector_parts(i):
                 nc.vector.scalar_tensor_tensor(
                     out=result[:, lo:hi], in0=gained[i][:, lo:hi], scalar=rstd[i][:],
@@ -315,17 +315,17 @@ def tile_multiheadattention_pb_kernel(
 
         first_addend = keep.tile([P, D], F32)
         second_addend = keep.tile([P, D], F32)
-        bias_sb = keep.tile([P, D], BF16)
+        bias_sb = keep.tile([P, BANK_BF], BF16)
         bias_ps = [spread.tile([P, BANK_BF], BF16, name="bias_ps%d" % h, tag="lo%d" % h) for h in range(2)]
 
-        def add_bias_first(half):
+        def add_bias(i, addend, half):
             cols = slice(half * BANK_BF, (half + 1) * BANK_BF)
             nc.vector.tensor_tensor(
-                out=first_addend[:, cols], in0=res_sb[:, FIRST, cols], in1=bias_ps[half][:], op=ALU.add
+                out=addend[:, cols], in0=res_sb[:, i, cols], in1=bias_ps[half][:], op=ALU.add
             )
 
-        def keep_bias(half):
-            nc.scalar.copy(out=bias_sb[:, half * BANK_BF : (half + 1) * BANK_BF], in_=bias_ps[half][:])
+        def keep_bias():
+            nc.scalar.copy(out=bias_sb[:], in_=bias_ps[0][:])
 
         flip_tokens([FIRST])
         gather_tokens([FIRST])
@@ -335,17 +335,17 @@ def tile_multiheadattention_pb_kernel(
         gather_tokens(group_tiles(0))
         turn_bias()
         quantise_tokens([FIRST])
-        add_bias_first(0)
-        keep_bias(0)
+        add_bias(FIRST, first_addend, 0)
+        keep_bias()
         quantise_tokens(group_tiles(0))
-        add_bias_first(1)
+        add_bias(FIRST, first_addend, 1)
         project(0)
-        keep_bias(1)
         direct(FIRST, 0, first_addend)
         direct(FIRST, 1, first_addend)
         project(1)
         direct(FIRST, 2, first_addend)
         direct(FIRST, 3, first_addend)
+        add_bias(SECOND, second_addend, 1)
         for tiles in ([SECOND], group_tiles(1), group_tiles(2)):
             flip_tokens(tiles)
         gather_tokens([SECOND], False)
@@ -358,8 +358,8 @@ def tile_multiheadattention_pb_kernel(
         middle.append(spread.tile([P, BANK_BF], BF16, name="middle"))
         for chunk in range(2):
             spread_row(gain_lo[0], chunk, norm_rows, chunk)
-        for part in range(8):
-            cols = slice(part * D // 8, (part + 1) * D // 8)
+        for part in range(4):
+            cols = slice(part * BANK_BF // 4, (part + 1) * BANK_BF // 4)
             nc.gpsimd.tensor_tensor(
                 out=second_addend[:, cols], in0=res_sb[:, SECOND, cols], in1=bias_sb[:, cols], op=ALU.add
             )

@@ -27,7 +27,7 @@ GROUP = GROUP_TILES * P
 GROUPS = (TILES - 2) // GROUP_TILES
 UNITS = GROUPS * CHUNKS
 LN_EPS = 1e-5
-POOL_COLS = (1024, 896, 768, 512)
+POOL_COLS = (1024, 896, 704, 512)
 POOL_ALONE = 5
 AHEAD = 2
 
@@ -131,9 +131,10 @@ def tile_multiheadattention_pb_kernel(
         x_turned = keep.tile([P, TILES * 4 * P], BF16, align_bytes=64)
         flipped = {}
 
-        def flip_tokens(tiles):
+        def flip_tokens(tiles, aside=False):
             key = tiles[0]
-            flipped[key] = by_token.tile([P, len(tiles), 2, P], F32, name="flipped", tag="turned")
+            pool, tag = (spread, "middle") if aside else (by_token, "turned")
+            flipped[key] = pool.tile([P, len(tiles), 2, P], F32, name="flipped", tag=tag)
             for a, i in enumerate(tiles):
                 x_words = x_sb[:, i, :].bitcast(F32)
                 for u in range(2):
@@ -342,20 +343,21 @@ def tile_multiheadattention_pb_kernel(
         project(0)
         direct(FIRST, 0, first_addend)
         direct(FIRST, 1, first_addend)
-        project(1)
         direct(FIRST, 2, first_addend)
+        project(1)
         direct(FIRST, 3, first_addend)
         add_bias(SECOND, second_addend, 1)
-        for tiles in ([SECOND], group_tiles(1), group_tiles(2)):
+        flip_tokens(group_tiles(1), True)
+        gather_tokens(group_tiles(1), True)
+        for tiles in ([SECOND], group_tiles(2)):
             flip_tokens(tiles)
-        gather_tokens([SECOND], False)
-        gather_tokens(group_tiles(1), False)
-        gather_tokens(group_tiles(2), True)
+        gather_tokens([SECOND], True)
+        gather_tokens(group_tiles(2), False)
         quantise_tokens([SECOND])
         quantise_tokens(group_tiles(1) + group_tiles(2))
         gain_lo.append(spread.tile([P, BANK_BF], BF16, name="gain_lo", tag="lo0"))
         shift_lo.append(spread.tile([P, BANK_BF], BF16, name="shift_lo", tag="lo1"))
-        middle.append(spread.tile([P, BANK_BF], BF16, name="middle"))
+        middle.append(spread.tile([P, BANK_BF], BF16, name="middle", tag="middle"))
         for chunk in range(2):
             spread_row(gain_lo[0], chunk, norm_rows, chunk)
         for part in range(4):
@@ -388,9 +390,11 @@ def tile_multiheadattention_pb_kernel(
         scale_shift_store(FIRST)
 
         for r in range(1, UNITS + 4):
+            if r == 1 and r + AHEAD < UNITS:
+                project(r + AHEAD)
             if r < UNITS:
                 add_residual(r)
-            if r + AHEAD < UNITS:
+            if not (r == 1) and r + AHEAD < UNITS:
                 project(r + AHEAD)
             if r < UNITS and r % CHUNKS == CHUNKS - 1:
                 for i in group_tiles(r // CHUNKS):

@@ -110,8 +110,8 @@ def tile_multiheadattention_pb_kernel(
         nc.sync.dma_start(
             out=norm_rows[CHUNKS : 2 * CHUNKS, :], in_=ln_b.rearrange("(c n) -> c n", n=BANK)
         )
-        load_x(SECOND)
         load_residual(SECOND)
+        load_x(SECOND)
         for i in range(4, TILES):
             load_x(i)
         for i in range(2, TILES):
@@ -330,10 +330,12 @@ def tile_multiheadattention_pb_kernel(
 
         flip_tokens([FIRST])
         gather_tokens([FIRST])
-        for chunk in range(CHUNKS):
-            spread_row(bias_ps[chunk // 2], chunk % 2, bias_chunks, chunk)
+        for chunk in range(CHUNKS // 2):
+            spread_row(bias_ps[0], chunk, bias_chunks, chunk)
         flip_tokens(group_tiles(0))
         gather_tokens(group_tiles(0))
+        for chunk in range(CHUNKS // 2):
+            spread_row(bias_ps[1], chunk, bias_chunks, CHUNKS // 2 + chunk)
         turn_bias()
         quantise_tokens([FIRST])
         add_bias(FIRST, first_addend, 0)

from concourse import mybir
from concourse.masks import make_identity

F32 = mybir.dt.float32
BF16 = mybir.dt.bfloat16
I32 = mybir.dt.int32
U32 = mybir.dt.uint32
U8 = mybir.dt.uint8
FP8X4 = mybir.dt.float8_e4m3fn_x4
FP4X4 = mybir.dt.float4_e2m1fn_x4
ALU = mybir.AluOpType
ACT = mybir.ActivationFunctionType

P = 128
TOKENS = 1024
HEADS = 4
K = 512
D = 2048
TILES = TOKENS // P
BANK = 512
BANK_BF = 2 * BANK
CHUNKS = D // BANK
BLOCKS = BANK // P
FIRST, SECOND = 0, 1
GROUP_TILES = 2
GROUP = GROUP_TILES * P
GROUPS = (TILES - 2) // GROUP_TILES
UNITS = GROUPS * CHUNKS
LN_EPS = 1e-5
POOL_COLS = (1024, 896, 704, 512)
POOL_ALONE = 5
AHEAD = 2

FLOPS = 2 * TOKENS * K * D


def tile_multiheadattention_pb_kernel(
    tc, attn_out, residual, proj_w_words, proj_w_scales, proj_b, ln_g, ln_b, out
):
    nc = tc.nc

    x_dram = attn_out.rearrange("h (p i) j -> i p h j", i=TILES)
    res_dram = residual.rearrange("(p i) d -> i p d", i=TILES)
    out_dram = out.rearrange("(p i) d -> i p d", i=TILES)

    with (
        tc.tile_pool(name="keep", bufs=1) as keep,
        tc.tile_pool(name="stage", bufs=2) as stage,
        tc.tile_pool(name="work", bufs=3) as work,
        tc.tile_pool(name="stats", bufs=TILES) as stats,
        tc.psum_pool(name="spread", bufs=1) as spread,
        tc.psum_pool(name="by_feature", bufs=2) as by_feature,
        tc.psum_pool(name="by_token", bufs=3) as by_token,
        tc.manual_schedule(),
    ):
        ident = keep.tile([P, P], F32)
        make_identity(nc, ident[:])
        bias_chunks = keep.tile([P, BANK], BF16)
        nc.vector.memset(bias_chunks[:].bitcast(I32), 0)
        w_plane = keep.tile([P, D], U8, align_bytes=64)
        nc.vector.memset(w_plane[:].bitcast(I32), 0)
        bias_rows = keep.tile([P, P], BF16)
        nc.vector.memset(bias_rows[:].bitcast(I32), 0)
        norm_rows = keep.tile([P, BANK], BF16)
        nc.vector.memset(norm_rows[:].bitcast(I32), 0)
        eps = keep.tile([P, 1], F32)
        nc.vector.memset(eps[:], LN_EPS)
        ident_bf = keep.tile([P, P], BF16)
        nc.vector.tensor_copy(out=ident_bf[:], in_=ident[:])

        nc.gpsimd.dma_start(out=bias_rows[0 : D // P, :], in_=proj_b.rearrange("(j p) -> j p", p=P))
        warm = keep.tile([P, 1], F32)
        nc.scalar.activation(out=warm[:], in_=eps[:], func=ACT.Abs_reciprocal_sqrt)

        x_sb = keep.tile([P, TILES, K], BF16)
        res_sb = keep.tile([P, TILES, D], BF16)
        w_words = keep.tile([P, 2 * D], U8, align_bytes=64)

        def load_x(i):
            nc.sync.dma_start(
                out=x_sb[:, i, :].rearrange("p (h j) -> p h j", h=HEADS), in_=x_dram[i]
            )

        def load_words(half):
            cols = slice(half * D, (half + 1) * D)
            nc.sync.dma_start(out=w_words[:, cols].bitcast(I32), in_=proj_w_words[0][:, cols].bitcast(I32))

        def load_residual(i, lo=0, hi=D):
            nc.sync.dma_start(out=res_sb[:, i, lo:hi], in_=res_dram[i][:, lo:hi])

        def load_scales():
            for quadrant in range(4):
                nc.sync.dma_start(
                    out=w_plane[32 * quadrant : 32 * quadrant + 4, :].bitcast(I32),
                    in_=proj_w_scales[0, 4 * quadrant : 4 * quadrant + 4, :].bitcast(I32),
                )

        load_x(FIRST)
        nc.sync.dma_start(
            out=bias_chunks[0:CHUNKS, :], in_=proj_b.rearrange("(c n) -> c n", n=BANK)
        )
        load_x(2)
        load_x(3)
        load_residual(FIRST, 0, BANK_BF)
        load_scales()
        load_words(0)
        load_residual(FIRST, BANK_BF, D)
        load_words(1)
        nc.sync.dma_start(out=norm_rows[0:CHUNKS, :], in_=ln_g.rearrange("(c n) -> c n", n=BANK))
        nc.sync.dma_start(
            out=norm_rows[CHUNKS : 2 * CHUNKS, :], in_=ln_b.rearrange("(c n) -> c n", n=BANK)
        )
        load_residual(SECOND)
        load_x(SECOND)
        for i in range(4, TILES):
            load_x(i)
        for i in range(2, TILES):
            load_residual(i)

        def spread_row(bank, part, rows, row):
            nc.tensor.matmul(
                out=bank[:, part * BANK : (part + 1) * BANK],
                lhsT=ident_bf[:, row : row + 1].to_broadcast([P, P]),
                rhs=rows[:],
                start=True,
                stop=True,
            )

        x_codes = keep.tile([P, TILES * P], U32, align_bytes=64)
        x_plane = keep.tile([P, TILES * P], U8, align_bytes=64)
        x_turned = keep.tile([P, TILES * 4 * P], BF16, align_bytes=64)
        flipped = {}

        def flip_tokens(tiles, aside=False):
            key = tiles[0]
            pool, tag = (spread, "middle") if aside else (by_token, "turned")
            flipped[key] = pool.tile([P, len(tiles), 2, P], F32, name="flipped", tag=tag)
            for a, i in enumerate(tiles):
                x_words = x_sb[:, i, :].bitcast(F32)
                for u in range(2):
                    nc.tensor.transpose(flipped[key][:, a, u, :], x_words[:, u : K // 2 : 2], ident[:])

        def gather_tokens(tiles, by_scalar=True):
            key = tiles[0]
            copy = nc.scalar.copy if by_scalar else nc.vector.tensor_copy
            copy(
                out=x_turned[:, key * 4 * P : (key + len(tiles)) * 4 * P].bitcast(F32).rearrange("p (a r u) -> p a r u", a=len(tiles), u=2),
                in_=flipped[key][:].rearrange("p a u r -> p a r u"),
            )

        def quantise_tokens(tiles):
            key = tiles[0]
            tokens = slice(key * P, (key + len(tiles)) * P)
            nc.vector.quantize_mx(
                out=x_codes[:, tokens].bitcast(FP8X4), scales=x_plane[:, tokens], in_=x_turned[:, key * 4 * P : (key + len(tiles)) * 4 * P],
            )

        def group_tiles(group):
            return [2 + group * GROUP_TILES + a for a in range(GROUP_TILES)]

        bias_cols = keep.tile([P, D // P], F32)
        biased = {}
        y = {}
        sums = {}
        neg_mean = {}
        rstd = {}
        gained = {}
        pooled = {}

        def turn_bias():
            bias_ps = by_feature.tile([P, P], BF16, tag="product")
            nc.tensor.transpose(bias_ps[:], bias_rows[:], ident_bf[:])
            nc.scalar.copy(out=bias_cols[:], in_=bias_ps[:, 0 : D // P])

        def add_chunk(i, chunk, product, addend):
            cols = slice(chunk * BANK, (chunk + 1) * BANK)
            if chunk == 0:
                y[i] = work.tile([P, D], F32, name="y", bufs=6)
                sums[i] = stats.tile([P, CHUNKS], F32, name="sums")
            nc.vector.scalar_tensor_tensor(
                out=y[i][:, cols], in0=product[:], scalar=0.0, in1=addend,
                op0=ALU.add, op1=ALU.add, accum_out=sums[i][:, chunk : chunk + 1],
            )

        def find_mean(i):
            scaled_sums = stats.tile([P, CHUNKS], F32, name="scaled_sums")
            neg_mean[i] = stats.tile([P, 1], F32, name="neg_mean")
            nc.scalar.activation(
                out=scaled_sums[:], in_=sums[i][:], func=ACT.Copy, scale=-1.0 / D,
                accum_out=neg_mean[i][:],
            )

        def direct(i, chunk, with_bias):
            cols = slice(chunk * BANK, (chunk + 1) * BANK)
            tokens = slice(i * P, (i + 1) * P)
            product = by_token.tile([P, BANK], F32, name="direct_product", tag="turned")
            nc.tensor.matmul_mx(
                out=product[:],
                lhsT=x_codes[:, tokens].bitcast(FP8X4),
                lhsT_scale=x_plane[:, tokens],
                rhs=w_words[:, 2 * chunk * BANK : 2 * (chunk + 1) * BANK].bitcast(FP4X4),
                rhs_scale=w_plane[:, cols],
                start=True,
                stop=True,
            )
            add_chunk(i, chunk, product, with_bias[:, cols])

        def project(unit):
            group, chunk = divmod(unit, CHUNKS)
            first = group_tiles(group)[0]
            tokens = slice(first * P, first * P + GROUP)
            biased[unit] = work.tile([P, BLOCKS, GROUP], F32, name="biased", bufs=AHEAD + 2)
            for pair in range(BLOCKS // 2):
                product = by_feature.tile([P, 2, GROUP], F32, tag="product")
                for e in range(2):
                    j = chunk * BLOCKS + 2 * pair + e
                    nc.tensor.matmul_mx(
                        out=product[:, e, :],
                        lhsT=w_words[:, 2 * j * P : 2 * (j + 1) * P].bitcast(FP4X4),
                        lhsT_scale=w_plane[:, j * P : (j + 1) * P],
                        rhs=x_codes[:, tokens].bitcast(FP8X4),
                        rhs_scale=x_plane[:, tokens],
                        start=True,
                        stop=True,
                    )
                for e in range(2):
                    j = chunk * BLOCKS + 2 * pair + e
                    nc.scalar.activation(
                        out=biased[unit][:, 2 * pair + e, :], in_=product[:, e, :], func=ACT.Identity,
                        bias=bias_cols[:, j : j + 1], scale=1.0,
                    )

        def add_residual(unit):
            group, chunk = divmod(unit, CHUNKS)
            for a, i in enumerate(group_tiles(group)):
                turned = by_token.tile([P, BANK], F32, tag="turned")
                for b in range(BLOCKS):
                    nc.tensor.transpose(
                        turned[:, b * P : (b + 1) * P], biased[unit][:, b, a * P : (a + 1) * P], ident[:]
                    )
                add_chunk(i, chunk, turned, res_sb[:, i, chunk * BANK : (chunk + 1) * BANK])

        gain_lo = []
        shift_lo = []
        middle = []
        pool_rows = keep.tile([P, 2, D - BANK_BF], BF16)

        def pool_cols(i):
            return POOL_COLS[i // 2]

        def vector_parts(i):
            parts = [(0, BANK_BF, gain_lo[0][:], shift_lo[0][:])]
            width = D - pool_cols(i) - BANK_BF
            if width > 0:
                parts.append(
                    (BANK_BF, BANK_BF + width, middle[0][:, 0:width], middle[0][:, BANK : BANK + width])
                )
            return parts

        def centre_and_gain(i):
            gained[i] = work.tile([P, D - POOL_COLS[3]], F32, name="gained")
            for lo, hi, gain, shift in vector_parts(i):
                nc.vector.scalar_tensor_tensor(
                    out=gained[i][:, lo:hi], in0=y[i][:, lo:hi], scalar=neg_mean[i][:],
                    in1=gain, op0=ALU.add, op1=ALU.mult,
                )

        def deviation(i):
            squares = stage.tile([P, D], BF16, name="squares")
            sum_sq = stats.tile([P, 1], F32, name="sum_sq")
            nc.scalar.activation(
                out=squares[:], in_=y[i][:], func=ACT.Square, bias=neg_mean[i][:], scale=1.0,
                accum_out=sum_sq[:],
            )
            rstd[i] = stats.tile([P, 1], F32, name="rstd")
            nc.scalar.activation(
                out=rstd[i][:], in_=sum_sq[:], func=ACT.Abs_reciprocal_sqrt, bias=eps[:], scale=1.0 / D
            )

        def pool_columns(i):
            pooled[i] = work.tile([P, POOL_COLS[0]], F32, name="pooled", bufs=5)
            first = D - pool_cols(i)
            mine = pooled[i][:, 0 : pool_cols(i)]
            if i < POOL_ALONE:
                nc.gpsimd.tensor_scalar(
                    out=mine, in0=y[i][:, first:D], scalar1=neg_mean[i][:], scalar2=rstd[i][:],
                    op0=ALU.add, op1=ALU.mult,
                )
            else:
                offset = stats.tile([P, 1], F32, name="offset")
                nc.scalar.activation(out=offset[:], in_=neg_mean[i][:], func=ACT.Copy, scale=rstd[i][:])
                nc.scalar.activation(
                    out=mine, in_=y[i][:, first:D], func=ACT.Identity, bias=offset[:], scale=rstd[i][:]
                )
            gain = pool_rows[:, 0, first - BANK_BF :]
            shift = pool_rows[:, 1, first - BANK_BF :]
            nc.gpsimd.tensor_tensor(out=mine, in0=mine, in1=gain, op=ALU.mult)
            nc.gpsimd.tensor_tensor(out=mine, in0=mine, in1=shift, op=ALU.add)

        def scale_shift_store(i):
            result = work.tile([P, D - POOL_COLS[3]], F32, name="result")
            for lo, hi, gain, shift in vector_parts(i):
                nc.vector.scalar_tensor_tensor(
                    out=result[:, lo:hi], in0=gained[i][:, lo:hi], scalar=rstd[i][:],
                    in1=shift, op0=ALU.mult, op1=ALU.add,
                )
                nc.sync.dma_start(out=out_dram[i][:, lo:hi], in_=result[:, lo:hi])

        def store_pooled(i):
            nc.sync.dma_start(out=out_dram[i][:, D - pool_cols(i) : D], in_=pooled[i][:, 0 : pool_cols(i)])

        def norm_first(i):
            centre_and_gain(i)
            deviation(i)
            pool_columns(i)

        first_addend = keep.tile([P, D], F32)
        second_addend = keep.tile([P, D], F32)
        bias_sb = keep.tile([P, BANK_BF], BF16)
        bias_ps = [spread.tile([P, BANK_BF], BF16, name="bias_ps%d" % h, tag="lo%d" % h) for h in range(2)]

        def add_bias(i, addend, half):
            cols = slice(half * BANK_BF, (half + 1) * BANK_BF)
            nc.vector.tensor_tensor(
                out=addend[:, cols], in0=res_sb[:, i, cols], in1=bias_ps[half][:], op=ALU.add
            )

        def keep_bias():
            nc.scalar.copy(out=bias_sb[:], in_=bias_ps[0][:])

        flip_tokens([FIRST])
        gather_tokens([FIRST])
        for chunk in range(CHUNKS // 2):
            spread_row(bias_ps[0], chunk, bias_chunks, chunk)
        flip_tokens(group_tiles(0))
        gather_tokens(group_tiles(0))
        for chunk in range(CHUNKS // 2):
            spread_row(bias_ps[1], chunk, bias_chunks, CHUNKS // 2 + chunk)
        turn_bias()
        quantise_tokens([FIRST])
        add_bias(FIRST, first_addend, 0)
        keep_bias()
        quantise_tokens(group_tiles(0))
        add_bias(FIRST, first_addend, 1)
        project(0)
        direct(FIRST, 0, first_addend)
        direct(FIRST, 1, first_addend)
        direct(FIRST, 2, first_addend)
        project(1)
        direct(FIRST, 3, first_addend)
        add_bias(SECOND, second_addend, 1)
        flip_tokens(group_tiles(1), True)
        gather_tokens(group_tiles(1), True)
        for tiles in ([SECOND], group_tiles(2)):
            flip_tokens(tiles)
        gather_tokens([SECOND], True)
        gather_tokens(group_tiles(2), False)
        quantise_tokens([SECOND])
        quantise_tokens(group_tiles(1) + group_tiles(2))
        gain_lo.append(spread.tile([P, BANK_BF], BF16, name="gain_lo", tag="lo0"))
        shift_lo.append(spread.tile([P, BANK_BF], BF16, name="shift_lo", tag="lo1"))
        middle.append(spread.tile([P, BANK_BF], BF16, name="middle", tag="middle"))
        for chunk in range(2):
            spread_row(gain_lo[0], chunk, norm_rows, chunk)
        for part in range(4):
            cols = slice(part * BANK_BF // 4, (part + 1) * BANK_BF // 4)
            nc.gpsimd.tensor_tensor(
                out=second_addend[:, cols], in0=res_sb[:, SECOND, cols], in1=bias_sb[:, cols], op=ALU.add
            )
        find_mean(FIRST)
        deviation(FIRST)
        add_residual(0)
        centre_and_gain(FIRST)
        for unit in range(2, AHEAD):
            project(unit)
        for chunk in range(2):
            spread_row(shift_lo[0], chunk, norm_rows, CHUNKS + chunk)
        top = by_token.tile([P, BANK_BF], BF16, name="top", tag="turned")
        for half, bank in enumerate([middle[0], top]):
            for vector in range(2):
                spread_row(bank, vector, norm_rows, vector * CHUNKS + 2 + half)
        for half, bank in enumerate([middle[0], top]):
            nc.scalar.copy(
                out=pool_rows[:, :, half * BANK : (half + 1) * BANK],
                in_=bank[:].rearrange("p (v n) -> p v n", n=BANK),
            )
        pool_columns(FIRST)
        for unit in range(AHEAD, AHEAD + 1):
            project(unit)
        for chunk in range(CHUNKS):
            direct(SECOND, chunk, second_addend)
        scale_shift_store(FIRST)

        for r in range(1, UNITS + 4):
            if r == 1 and r + AHEAD < UNITS:
                project(r + AHEAD)
            if r < UNITS:
                add_residual(r)
            if not (r == 1) and r + AHEAD < UNITS:
                project(r + AHEAD)
            if r < UNITS and r % CHUNKS == CHUNKS - 1:
                for i in group_tiles(r // CHUNKS):
                    find_mean(i)
            if r == 1:
                find_mean(SECOND)
                norm_first(SECOND)
                store_pooled(FIRST)
            if r == 2:
                scale_shift_store(SECOND)
            if r == 3:
                store_pooled(SECOND)
            group, step = divmod(r - CHUNKS, CHUNKS)
            if 0 <= group < GROUPS:
                first, second = group_tiles(group)
                if step == 0:
                    norm_first(first)
                if step == 1:
                    norm_first(second)
                if step == 2:
                    scale_shift_store(first)
                    store_pooled(first)
                if step == 3:
                    scale_shift_store(second)
                    store_pooled(second)
